import numpy as np
import ml_dtypes


def mxq(x, axis, fmt="e4m3"):
    dtype, down = {"e4m3": (ml_dtypes.float8_e4m3fn, 7), "e5m2": (ml_dtypes.float8_e5m2, 14)}[fmt]
    v = np.moveaxis(np.asarray(x, np.float32).astype(ml_dtypes.bfloat16).astype(np.float64), axis, -1)
    blocks = v.reshape(v.shape[:-1] + (-1, 32))
    amax = np.abs(blocks).max(-1, keepdims=True)
    byte = np.maximum(np.where(amax > 0, np.frexp(amax)[1] - 1 + 127, 0) - down, 1)
    scale = np.exp2(byte - 127.0)
    codes = (blocks / scale).astype(np.float32).astype(dtype).astype(np.float64)
    return np.moveaxis((codes * scale).reshape(v.shape), -1, axis)


WIDE = False


def mx_kscale(k):
    if not WIDE:
        return np.ones(k)
    levels = np.array([10, -10, 5, -5, 0])
    a = np.random.permutation(np.resize(levels, k // 512 * 4)).reshape(k // 512, 4)
    idx = np.arange(k)
    return np.exp2(a[idx // 512, idx % 128 // 32])


BF16 = ml_dtypes.bfloat16


def bf(x):
    return np.asarray(x, np.float32).astype(BF16)


def f64(x):
    return np.asarray(x).astype(np.float64)


E2M1 = np.array([0.0, 0.5, 1.0, 1.5, 2.0, 3.0, 4.0, 6.0, -0.0, -0.5, -1.0, -1.5, -2.0, -3.0, -4.0, -6.0])


def pack_weight(w, fmt):
    k, n = w.shape
    w = f64(bf(w)).reshape(k // 32, 32, n)
    amax = np.abs(w).max(1)
    if fmt == "e4m3":
        byte = np.frexp(amax)[1] - 1 + 127 - 7
    else:
        mant, ex = np.frexp(amax / 6.0)
        byte = np.where(mant > 0.5, ex, ex - 1) + 127
    byte = np.clip(np.where(amax > 0, byte, 1), 1, 254)
    scaled = (w * np.exp2(127.0 - byte)[:, None, :]).reshape(k, n).astype(np.float32)
    by_word = np.ascontiguousarray(scaled.reshape(k // 512, 128, 4, n).transpose(0, 1, 3, 2))
    if fmt == "e4m3":
        words = by_word.astype(ml_dtypes.float8_e4m3fn).view(np.uint8)
    else:
        c = by_word.astype(ml_dtypes.float4_e2m1fn).view(np.uint8) & 0xF
        words = c[..., 0::2] | (c[..., 1::2] << 4)
    return np.ascontiguousarray(words), np.ascontiguousarray(byte.astype(np.uint8).reshape(k // 512, 16, n))


def unpack_weight(words, scales, fmt):
    g, p, n, _ = words.shape
    if fmt == "e4m3":
        vals = np.ascontiguousarray(words).view(ml_dtypes.float8_e4m3fn).astype(np.float64)
    else:
        nib = np.empty((g, p, n, 4), np.uint8)
        nib[..., 0::2] = words & 0xF
        nib[..., 1::2] = words >> 4
        vals = E2M1[nib]
    vals = vals * np.repeat(np.exp2(scales.astype(np.float64) - 127.0), 8, axis=1)[..., None]
    return vals.transpose(0, 1, 3, 2).reshape(g * 512, n)

def pack4(w):
    words, scales = pack_weight(w, "e2m1")
    return words.reshape(words.shape[0], 128, -1), scales


def unpack4(words, scales):
    return unpack_weight(words.reshape(words.shape[0], 128, -1, 2), scales, "e2m1")


B, S, D = 4, 512, 1024
NB = 2
W = 2 * NB + 1


def setup_inputs():
    s = mx_kscale(D)
    x = bf(np.random.standard_normal((B, S, D)) * s)
    wq = np.random.standard_normal((D, D)) / np.sqrt(D) / s[None, :]
    Wq_words, Wq_scales = pack4(wq.T)
    bq = bf(np.random.standard_normal(D) * 0.3)
    k_proj = bf(np.random.standard_normal((B, S, D)))
    return {"x": x,
            "Wq_words": Wq_words,
            "Wq_scales": Wq_scales,
            "bq": bq,
            "k_proj": k_proj}


def reference(x, Wq_words, Wq_scales, bq, k_proj):
    kf = f64(k_proj)
    q = (mxq(f64(x), 2, "e4m3") @ unpack4(Wq_words, Wq_scales)) + f64(bq)
    scores = np.full((B, S, W), -np.inf)
    for j in range(W):
        o = j - NB
        lo, hi = max(0, -o), S - max(0, o)
        scores[:, lo:hi, j] = (q[:, lo:hi] * kf[:, lo + o:hi + o]).sum(-1) / np.sqrt(D)
    e = np.exp(scores - scores.max(-1, keepdims=True))
    return e / e.sum(-1, keepdims=True)

@@ -1,0 +1,223 @@
+import math
+
+import concourse.mybir as mybir
+from concourse.masks import make_identity
+
+BF16 = mybir.dt.bfloat16
+F32 = mybir.dt.float32
+I32 = mybir.dt.int32
+U8 = mybir.dt.uint8
+U32 = mybir.dt.uint32
+FP8X4 = mybir.dt.float8_e4m3fn_x4
+FP4X4 = mybir.dt.float4_e2m1fn_x4
+ACT = mybir.ActivationFunctionType
+ALU = mybir.AluOpType
+AXIS = mybir.AxisListType
+
+P = 128
+BATCHES, SEQ, D = 4, 512, 1024
+TOKENS = BATCHES * SEQ
+NB = 2
+BAND = 2 * NB + 1
+RUN = TOKENS // P
+SLOTS = RUN + 2 * NB
+PARTS_PER_BATCH = SEQ // RUN
+PACK = 4
+K_PASS = P * PACK
+PASSES = D // K_PASS
+CHUNKS = D // P
+BANK = 512
+HALVES = D // BANK
+GROUP = BANK // P
+GROUPS = RUN // GROUP
+SCORE_SCALE = 1.0 / math.sqrt(D)
+MASKED = -1.0e30
+HALO_CUT = 112
+
+FLOPS = 2 * TOKENS * D * D + 2 * TOKENS * BAND * D
+
+
+def tile_crosssliceattention_pa_kernel(tc, x, Wq_words, Wq_scales, bq, k_proj, out):
+    nc = tc.nc
+    x_runs = x.flatten_outer_dims().rearrange("(p i) k -> p i k", i=RUN)
+    k_runs = k_proj.flatten_outer_dims().rearrange("(p i) d -> p i d", i=RUN)
+    out_runs = out.flatten_outer_dims().rearrange("(p i) j -> p (i j)", i=RUN)
+
+    with tc.tile_pool(name="keep", bufs=1) as keep, tc.tile_pool(name="work", bufs=2) as work, tc.psum_pool(
+        name="psum", bufs=2
+    ) as psum:
+        x_sb = keep.tile([P, RUN, D], BF16)
+        k_sb = keep.tile([P, SLOTS, D], BF16)
+        w_words = keep.tile([P, PASSES, 2 * D], U8, align_bytes=64)
+        w_planes = keep.tile([P, PASSES, D], U8, align_bytes=64)
+        bias_raw = keep.tile([CHUNKS, P], BF16)
+
+        nc.vector.memset(w_planes[:].bitcast(I32), 0)
+        nc.vector.memset(k_sb[0:1, 0:NB, :], 0.0)
+        nc.vector.memset(k_sb[P - 32 : P, SLOTS - NB : SLOTS, :], 0.0)
+
+        def load_x(t):
+            tiles = slice(GROUP * t, GROUP * (t + 1))
+            nc.sync.dma_start(out=x_sb[:, tiles, :], in_=x_runs[:, tiles, :])
+
+        def load_k(t):
+            nc.sync.dma_start(
+                out=k_sb[:, NB + GROUP * t : NB + GROUP * (t + 1), :],
+                in_=k_runs[:, GROUP * t : GROUP * (t + 1), :],
+            )
+
+        load_x(0)
+        nc.sync.dma_start(
+            out=w_words[:].bitcast(I32), in_=Wq_words.rearrange("g p b -> p g b").bitcast(I32)
+        )
+        for quad in range(4):
+            nc.sync.dma_start(
+                out=w_planes[32 * quad : 32 * quad + 4].bitcast(I32),
+                in_=Wq_scales[:, 4 * quad : 4 * quad + 4, :].rearrange("g r n -> r g n").bitcast(I32),
+            )
+        nc.sync.dma_start(out=bias_raw[:], in_=bq.rearrange("(c f) -> c f", f=P))
+        cut = P - HALO_CUT
+        nc.sync.dma_start(out=k_sb[1:cut, 0:NB, :], in_=k_runs[0 : cut - 1, RUN - NB : RUN, :])
+        nc.sync.dma_start(out=k_sb[cut:P, 0:NB, :], in_=k_runs[cut - 1 : P - 1, RUN - NB : RUN, :])
+        load_k(0)
+        load_k(1)
+        for t in range(1, GROUPS):
+            load_x(t)
+            if t + 1 < GROUPS:
+                load_k(t + 1)
+        nc.sync.dma_start(
+            out=k_sb[0:HALO_CUT, SLOTS - NB : SLOTS, :], in_=k_runs[1 : HALO_CUT + 1, 0:NB, :]
+        )
+        nc.sync.dma_start(
+            out=k_sb[HALO_CUT : P - 1, SLOTS - NB : SLOTS, :], in_=k_runs[HALO_CUT + 1 : P, 0:NB, :]
+        )
+
+        ident = keep.tile([P, P], F32)
+        make_identity(nc, ident[:])
+
+        warm = keep.tile([P, 1], F32)
+        nc.vector.memset(warm[:], 0.0)
+        nc.scalar.activation(out=warm[:], in_=warm[:], func=ACT.Exp)
+
+        bias_rows = keep.tile([P, P], F32)
+        nc.vector.memset(bias_rows[:], 0.0)
+        nc.vector.tensor_scalar_mul(out=bias_rows[0:CHUNKS, :], in0=bias_raw[:], scalar1=SCORE_SCALE)
+        bias_ps = psum.tile([P, P], F32, tag="xT")
+        nc.tensor.transpose(bias_ps[:], bias_rows[:], ident[:])
+        bias_col = keep.tile([P, CHUNKS], F32)
+        nc.vector.tensor_copy(out=bias_col[:], in_=bias_ps[:, 0:CHUNKS])
+
+        ident_by_batch = ident[:].rearrange("p (b r) -> p b r", r=PARTS_PER_BATCH)
+        starts = keep.tile([P, 1], F32)
+        ends = keep.tile([P, 1], F32)
+        nc.vector.tensor_reduce(out=starts[:], in_=ident_by_batch[:, :, 0], axis=AXIS.X, op=ALU.add)
+        nc.vector.tensor_reduce(
+            out=ends[:], in_=ident_by_batch[:, :, PARTS_PER_BATCH - 1], axis=AXIS.X, op=ALU.add
+        )
+        edge_mask = keep.tile([P, RUN, BAND], F32)
+        nc.vector.memset(edge_mask[:], 0.0)
+        for i in range(NB):
+            missing = NB - i
+            nc.vector.tensor_scalar_mul(
+                out=edge_mask[:, i, 0:missing], in0=starts[:].to_broadcast([P, missing]), scalar1=MASKED
+            )
+            nc.vector.tensor_scalar_mul(
+                out=edge_mask[:, RUN - 1 - i, BAND - missing : BAND],
+                in0=ends[:].to_broadcast([P, missing]),
+                scalar1=MASKED,
+            )
+
+        sums = keep.tile([P, RUN, BAND, HALVES], F32)
+
+        def quantise_group(t):
+            grouped = work.tile([P, PASSES, BANK, PACK], BF16, align_bytes=64)
+            grouped_pairs = grouped[:].bitcast(F32)
+            for m in range(GROUP):
+                x_pairs = x_sb[:, GROUP * t + m, :].bitcast(F32)
+                xT = psum.tile([P, PASSES, 2, P], F32, tag="xT")
+                for g in range(PASSES):
+                    for u in range(2):
+                        first = (K_PASS // 2) * g + u
+                        nc.tensor.transpose(
+                            xT[:, g, u, :], x_pairs[:, first : (K_PASS // 2) * (g + 1) : 2], ident[:]
+                        )
+                nc.scalar.copy(
+                    out=grouped_pairs[:, :, P * m : P * (m + 1), :],
+                    in_=xT[:].rearrange("p g u m -> p g m u"),
+                )
+            codes = work.tile([P, PASSES, BANK], U32, align_bytes=64)
+            planes = work.tile([P, PASSES, BANK], U8, align_bytes=64)
+            nc.vector.quantize_mx(
+                out=codes[:].rearrange("p g m -> p (g m)").bitcast(FP8X4),
+                scales=planes[:].rearrange("p g m -> p (g m)"),
+                in_=grouped[:].rearrange("p g m t -> p (g m t)"),
+            )
+            return codes, planes
+
+        def project_group(codes, planes):
+            qT = work.tile([P, CHUNKS, BANK], F32)
+            for c in range(CHUNKS):
+                acc = psum.tile([P, BANK], F32, tag="acc")
+                for g in range(PASSES):
+                    nc.tensor.matmul_mx(
+                        out=acc[:],
+                        lhsT=w_words[:, g, 2 * P * c : 2 * P * (c + 1)].bitcast(FP4X4),
+                        lhsT_scale=w_planes[:, g, P * c : P * (c + 1)],
+                        rhs=codes[:, g, :].bitcast(FP8X4),
+                        rhs_scale=planes[:, g, :],
+                        start=(g == 0),
+                        stop=(g == PASSES - 1),
+                    )
+                nc.scalar.activation(
+                    out=qT[:, c, :],
+                    in_=acc[:],
+                    func=ACT.Identity,
+                    bias=bias_col[:, c : c + 1],
+                    scale=SCORE_SCALE,
+                )
+            return qT
+
+        def band_scores(i, qT, m):
+            for h in range(HALVES):
+                q = psum.tile([P, BANK], F32, tag="q", bufs=4)
+                for c in range(GROUP):
+                    nc.tensor.transpose(
+                        q[:, P * c : P * (c + 1)], qT[:, GROUP * h + c, P * m : P * (m + 1)], ident[:]
+                    )
+                for j in range(BAND):
+                    products = work.tile([P, BANK], F32, bufs=4)
+                    nc.vector.scalar_tensor_tensor(
+                        out=products[:],
+                        in0=q[:],
+                        scalar=1.0,
+                        in1=k_sb[:, i + j, BANK * h : BANK * (h + 1)],
+                        op0=ALU.mult,
+                        op1=ALU.mult,
+                        accum_out=sums[:, i, j, h : h + 1],
+                    )
+
+        staged = quantise_group(0)
+        for t in range(GROUPS):
+            qT = project_group(staged[0], staged[1])
+            if t + 1 < GROUPS:
+                staged = quantise_group(t + 1)
+            for m in range(GROUP):
+                band_scores(GROUP * t + m, qT, m)
+
+        scores = keep.tile([P, RUN, BAND], F32)
+        nc.vector.tensor_reduce(out=scores[:], in_=sums[:], axis=AXIS.X, op=ALU.add)
+        nc.vector.tensor_add(out=scores[:], in0=scores[:], in1=edge_mask[:])
+        top = keep.tile([P, RUN], F32)
+        nc.vector.tensor_reduce(out=top[:], in_=scores[:], axis=AXIS.X, op=ALU.max)
+        nc.vector.tensor_sub(
+            out=scores[:], in0=scores[:], in1=top[:].unsqueeze(2).to_broadcast([P, RUN, BAND])
+        )
+        weights = keep.tile([P, RUN, BAND], F32)
+        nc.scalar.activation(out=weights[:], in_=scores[:], func=ACT.Exp)
+        total = keep.tile([P, RUN], F32)
+        nc.vector.tensor_reduce(out=total[:], in_=weights[:], axis=AXIS.X, op=ALU.add)
+        nc.vector.reciprocal(out=total[:], in_=total[:])
+        nc.vector.tensor_mul(
+            out=weights[:], in0=weights[:], in1=total[:].unsqueeze(2).to_broadcast([P, RUN, BAND])
+        )
+        nc.sync.dma_start(out=out_runs, in_=weights[:].rearrange("p i j -> p (i j)"))

@@ -16,57 +16,71 @@ AXIS = mybir.AxisListType
 
 P = 128
 BATCHES, SEQ, D = 4, 512, 1024
-TOKENS = BATCHES * SEQ
 NB = 2
 BAND = 2 * NB + 1
-RUN = TOKENS // P
+TILES = SEQ // P
+RUN = SEQ // P
 SLOTS = RUN + 2 * NB
-PARTS_PER_BATCH = SEQ // RUN
 PACK = 4
 K_PASS = P * PACK
 PASSES = D // K_PASS
 CHUNKS = D // P
 BANK = 512
 HALVES = D // BANK
-GROUP = BANK // P
-GROUPS = RUN // GROUP
+PAD = 8
+WINDOW = P + 2 * NB
+FOLDS = -(-WINDOW // BAND)
+PAIR = 2
 SCORE_SCALE = 1.0 / math.sqrt(D)
 MASKED = -1.0e30
 HALO_CUT = 112
+PRODUCTS_PER_BLOCK = 2
 
-FLOPS = 2 * TOKENS * D * D + 2 * TOKENS * BAND * D
+FLOPS = 2 * BATCHES * SEQ * D * D + 2 * BATCHES * SEQ * BAND * D
 
 
 def tile_crosssliceattention_pa_kernel(tc, x, Wq_words, Wq_scales, bq, k_proj, out):
     nc = tc.nc
-    x_runs = x.flatten_outer_dims().rearrange("(p i) k -> p i k", i=RUN)
-    k_runs = k_proj.flatten_outer_dims().rearrange("(p i) d -> p i d", i=RUN)
-    out_runs = out.flatten_outer_dims().rearrange("(p i) j -> p (i j)", i=RUN)
 
     with tc.tile_pool(name="keep", bufs=1) as keep, tc.tile_pool(name="work", bufs=2) as work, tc.psum_pool(
         name="psum", bufs=2
     ) as psum:
-        x_sb = keep.tile([P, RUN, D], BF16)
-        k_sb = keep.tile([P, SLOTS, D], BF16)
+        x_sb = keep.tile([P, BATCHES, TILES, D], BF16)
+        k_run = keep.tile([P, SLOTS, D], BF16)
+        k_sb = keep.tile([P, BATCHES - 1, TILES, D], BF16)
         w_words = keep.tile([P, PASSES, 2 * D], U8, align_bytes=64)
         w_planes = keep.tile([P, PASSES, D], U8, align_bytes=64)
         bias_raw = keep.tile([CHUNKS, P], BF16)
 
         nc.vector.memset(w_planes[:].bitcast(I32), 0)
-        nc.vector.memset(k_sb[0:1, 0:NB, :], 0.0)
-        nc.vector.memset(k_sb[P - 32 : P, SLOTS - NB : SLOTS, :], 0.0)
+        nc.vector.memset(k_run[0:1, 0:NB, :], 0.0)
+        nc.vector.memset(k_run[P - 32 : P, SLOTS - NB : SLOTS, :], 0.0)
 
-        def load_x(t):
-            tiles = slice(GROUP * t, GROUP * (t + 1))
-            nc.sync.dma_start(out=x_sb[:, tiles, :], in_=x_runs[:, tiles, :])
+        def load_x(b):
+            if b == 0:
+                tiles = x[b].rearrange("(p i) k -> p i k", i=RUN)
+            else:
+                tiles = x[b].rearrange("(n p) k -> p n k", p=P)
+            for m in range(TILES):
+                nc.sync.dma_start(out=x_sb[:, b, m, :], in_=tiles[:, m, :])
 
-        def load_k(t):
+        def load_k(b):
+            nc.sync.dma_start(out=k_sb[:, b - 1, :, :], in_=k_proj[b].rearrange("(n p) d -> p n d", p=P))
+
+        def load_k_run():
+            runs = k_proj[0].rearrange("(p i) d -> p i d", i=RUN)
+            nc.sync.dma_start(out=k_run[:, NB : NB + RUN, :], in_=runs)
+            cut = P - HALO_CUT
+            nc.sync.dma_start(out=k_run[1:cut, 0:NB, :], in_=runs[0 : cut - 1, RUN - NB : RUN, :])
+            nc.sync.dma_start(out=k_run[cut:P, 0:NB, :], in_=runs[cut - 1 : P - 1, RUN - NB : RUN, :])
+            nc.sync.dma_start(out=k_run[0:HALO_CUT, SLOTS - NB : SLOTS, :], in_=runs[1 : HALO_CUT + 1, 0:NB, :])
             nc.sync.dma_start(
-                out=k_sb[:, NB + GROUP * t : NB + GROUP * (t + 1), :],
-                in_=k_runs[:, GROUP * t : GROUP * (t + 1), :],
+                out=k_run[HALO_CUT : P - 1, SLOTS - NB : SLOTS, :], in_=runs[HALO_CUT + 1 : P, 0:NB, :]
             )
 
+        nc.sync.dma_start(out=bias_raw[:], in_=bq.rearrange("(c f) -> c f", f=P))
         load_x(0)
+        load_x(1)
         nc.sync.dma_start(
             out=w_words[:].bitcast(I32), in_=Wq_words.rearrange("g p b -> p g b").bitcast(I32)
         )
@@ -75,25 +89,16 @@ def tile_crosssliceattention_pa_kernel(tc, x, Wq_words, Wq_scales, bq, k_proj, o
                 out=w_planes[32 * quad : 32 * quad + 4].bitcast(I32),
                 in_=Wq_scales[:, 4 * quad : 4 * quad + 4, :].rearrange("g r n -> r g n").bitcast(I32),
             )
-        nc.sync.dma_start(out=bias_raw[:], in_=bq.rearrange("(c f) -> c f", f=P))
-        cut = P - HALO_CUT
-        nc.sync.dma_start(out=k_sb[1:cut, 0:NB, :], in_=k_runs[0 : cut - 1, RUN - NB : RUN, :])
-        nc.sync.dma_start(out=k_sb[cut:P, 0:NB, :], in_=k_runs[cut - 1 : P - 1, RUN - NB : RUN, :])
-        load_k(0)
         load_k(1)
-        for t in range(1, GROUPS):
-            load_x(t)
-            if t + 1 < GROUPS:
-                load_k(t + 1)
-        nc.sync.dma_start(
-            out=k_sb[0:HALO_CUT, SLOTS - NB : SLOTS, :], in_=k_runs[1 : HALO_CUT + 1, 0:NB, :]
-        )
-        nc.sync.dma_start(
-            out=k_sb[HALO_CUT : P - 1, SLOTS - NB : SLOTS, :], in_=k_runs[HALO_CUT + 1 : P, 0:NB, :]
-        )
+        load_k_run()
+        for b in range(2, BATCHES):
+            load_x(b)
+            load_k(b)
 
         ident = keep.tile([P, P], F32)
         make_identity(nc, ident[:])
+        ident_bf = keep.tile([P, P], BF16)
+        make_identity(nc, ident_bf[:])
 
         warm = keep.tile([P, 1], F32)
         nc.vector.memset(warm[:], 0.0)
@@ -107,33 +112,56 @@ def tile_crosssliceattention_pa_kernel(tc, x, Wq_words, Wq_scales, bq, k_proj, o
         bias_col = keep.tile([P, CHUNKS], F32)
         nc.vector.tensor_copy(out=bias_col[:], in_=bias_ps[:, 0:CHUNKS])
 
-        ident_by_batch = ident[:].rearrange("p (b r) -> p b r", r=PARTS_PER_BATCH)
-        starts = keep.tile([P, 1], F32)
-        ends = keep.tile([P, 1], F32)
-        nc.vector.tensor_reduce(out=starts[:], in_=ident_by_batch[:, :, 0], axis=AXIS.X, op=ALU.add)
-        nc.vector.tensor_reduce(
-            out=ends[:], in_=ident_by_batch[:, :, PARTS_PER_BATCH - 1], axis=AXIS.X, op=ALU.add
+        pick = keep.tile([P, PAIR, P], F32)
+        nc.vector.memset(pick[:], 0.0)
+        nc.vector.tensor_copy(
+            out=pick[:, :, 0 : P // PAIR], in_=ident[:].rearrange("p (m e) -> p e m", e=PAIR)
         )
-        edge_mask = keep.tile([P, RUN, BAND], F32)
-        nc.vector.memset(edge_mask[:], 0.0)
+
+        run_mask = keep.tile([P, RUN, BAND], F32)
+        block_mask = keep.tile([P, TILES, BAND], F32)
+        nc.vector.memset(run_mask[:], 0.0)
+        nc.vector.memset(block_mask[:], 0.0)
         for i in range(NB):
             missing = NB - i
             nc.vector.tensor_scalar_mul(
-                out=edge_mask[:, i, 0:missing], in0=starts[:].to_broadcast([P, missing]), scalar1=MASKED
+                out=run_mask[:, i, 0:missing], in0=ident[:, 0:1].to_broadcast([P, missing]), scalar1=MASKED
             )
             nc.vector.tensor_scalar_mul(
-                out=edge_mask[:, RUN - 1 - i, BAND - missing : BAND],
-                in0=ends[:].to_broadcast([P, missing]),
+                out=run_mask[:, RUN - 1 - i, BAND - missing : BAND],
+                in0=ident[:, P - 1 : P].to_broadcast([P, missing]),
                 scalar1=MASKED,
             )
+            for columns, partition in (
+                (block_mask[:, 0, 0:missing], i),
+                (block_mask[:, TILES - 1, BAND - missing : BAND], P - 1 - i),
+            ):
+                nc.vector.scalar_tensor_tensor(
+                    out=columns,
+                    in0=ident[:, partition : partition + 1].to_broadcast([P, missing]),
+                    scalar=MASKED,
+                    in1=columns,
+                    op0=ALU.mult,
+                    op1=ALU.add,
+                )
 
-        sums = keep.tile([P, RUN, BAND, HALVES], F32)
+        in_band = keep.tile([P, WINDOW], F32)
+        nc.vector.memset(in_band[:], 0.0)
+        for j in range(BAND):
+            nc.vector.tensor_add(out=in_band[:, j : j + P], in0=in_band[:, j : j + P], in1=ident[:])
+        banded = keep.tile([P, TILES, FOLDS * BAND], F32)
+        nc.vector.memset(banded[:], 0.0)
+        turn = keep.tile([P, BAND], F32)
+        nc.vector.tensor_copy(out=banded[:, 0, 0:P], in_=ident[:])
+        nc.vector.tensor_reduce(
+            out=turn[:], in_=banded[:, 0, :].rearrange("p (a r) -> p r a", r=BAND), axis=AXIS.X, op=ALU.add
+        )
 
-        def quantise_group(t):
-            grouped = work.tile([P, PASSES, BANK, PACK], BF16, align_bytes=64)
+        def quantise_batch(b):
+            grouped = work.tile([P, PASSES, SEQ, PACK], BF16, align_bytes=64)
             grouped_pairs = grouped[:].bitcast(F32)
-            for m in range(GROUP):
-                x_pairs = x_sb[:, GROUP * t + m, :].bitcast(F32)
+            for m in range(TILES):
+                x_pairs = x_sb[:, b, m, :].bitcast(F32)
                 xT = psum.tile([P, PASSES, 2, P], F32, tag="xT")
                 for g in range(PASSES):
                     for u in range(2):
@@ -145,8 +173,8 @@ def tile_crosssliceattention_pa_kernel(tc, x, Wq_words, Wq_scales, bq, k_proj, o
                     out=grouped_pairs[:, :, P * m : P * (m + 1), :],
                     in_=xT[:].rearrange("p g u m -> p g m u"),
                 )
-            codes = work.tile([P, PASSES, BANK], U32, align_bytes=64)
-            planes = work.tile([P, PASSES, BANK], U8, align_bytes=64)
+            codes = work.tile([P, PASSES, SEQ], U32, align_bytes=64)
+            planes = work.tile([P, PASSES, SEQ], U8, align_bytes=64)
             nc.vector.quantize_mx(
                 out=codes[:].rearrange("p g m -> p (g m)").bitcast(FP8X4),
                 scales=planes[:].rearrange("p g m -> p (g m)"),
@@ -154,10 +182,10 @@ def tile_crosssliceattention_pa_kernel(tc, x, Wq_words, Wq_scales, bq, k_proj, o
             )
             return codes, planes
 
-        def project_group(codes, planes):
-            qT = work.tile([P, CHUNKS, BANK], F32)
+        def project_batch(codes, planes):
+            qT = work.tile([P, CHUNKS, SEQ], F32)
             for c in range(CHUNKS):
-                acc = psum.tile([P, BANK], F32, tag="acc")
+                acc = psum.tile([P, SEQ], F32, tag="acc")
                 for g in range(PASSES):
                     nc.tensor.matmul_mx(
                         out=acc[:],
@@ -177,47 +205,148 @@ def tile_crosssliceattention_pa_kernel(tc, x, Wq_words, Wq_scales, bq, k_proj, o
                 )
             return qT
 
-        def band_scores(i, qT, m):
+        def new_keys():
+            kT = work.tile([P, CHUNKS, PAD + SEQ + PAD], F32)
+            nc.gpsimd.memset(kT[:, :, 0:PAD], 0.0)
+            nc.gpsimd.memset(kT[:, :, PAD + SEQ : PAD + SEQ + PAD], 0.0)
+            return kT
+
+        def transpose_keys(kT, b, n):
+            kT_ps = psum.tile([P, CHUNKS, P], BF16, tag="kT")
+            for c in range(CHUNKS):
+                nc.tensor.transpose(kT_ps[:, c, :], k_sb[:, b - 1, n, P * c : P * (c + 1)], ident_bf[:])
+            nc.scalar.copy(out=kT[:, :, PAD + P * n : PAD + P * (n + 1)], in_=kT_ps[:])
+
+        def softmax_rows(scores, mask):
+            rows = [P, scores.shape[1]]
+            nc.vector.tensor_add(out=scores[:], in0=scores[:], in1=mask[:])
+            top = work.tile(rows, F32)
+            nc.vector.tensor_reduce(out=top[:], in_=scores[:], axis=AXIS.X, op=ALU.max)
+            nc.vector.tensor_sub(
+                out=scores[:], in0=scores[:], in1=top[:].unsqueeze(2).to_broadcast(rows + [BAND])
+            )
+            weights = work.tile(rows + [BAND], F32)
+            nc.scalar.activation(out=weights[:], in_=scores[:], func=ACT.Exp)
+            total = work.tile(rows, F32)
+            nc.vector.tensor_reduce(out=total[:], in_=weights[:], axis=AXIS.X, op=ALU.add)
+            nc.vector.reciprocal(out=total[:], in_=total[:])
+            nc.vector.tensor_mul(
+                out=weights[:], in0=weights[:], in1=total[:].unsqueeze(2).to_broadcast(rows + [BAND])
+            )
+            return weights
+
+        def band_block(qT, kT, n):
+            block = psum.tile([P, WINDOW], F32, tag="block")
+            first_key = PAD - NB + P * n
+            for c in range(CHUNKS):
+                nc.tensor.matmul(
+                    out=block[:],
+                    lhsT=qT[:, c, P * n : P * (n + 1)],
+                    rhs=kT[:, c, first_key : first_key + WINDOW],
+                    start=(c == 0),
+                    stop=(c == CHUNKS - 1),
+                )
+            nc.vector.tensor_mul(out=banded[:, n, 0:WINDOW], in0=block[:], in1=in_band[:])
+
+        def band_scores():
+            folded = work.tile([P, TILES, 2, BAND], F32)
+            nc.vector.tensor_reduce(
+                out=folded[:, :, 0, :],
+                in_=banded[:].rearrange("p n (a r) -> p n r a", r=BAND),
+                axis=AXIS.X,
+                op=ALU.add,
+            )
+            nc.vector.tensor_copy(out=folded[:, :, 1, :], in_=folded[:, :, 0, :])
+            twice = folded[:].rearrange("p n t r -> p n (t r)")
+            scores = work.tile([P, TILES, BAND], F32)
+            nc.vector.tensor_scalar_mul(out=scores[:], in0=twice[:, :, 0:BAND], scalar1=turn[:, 0:1])
+            for s in range(1, BAND):
+                nc.vector.scalar_tensor_tensor(
+                    out=scores[:],
+                    in0=twice[:, :, s : s + BAND],
+                    scalar=turn[:, s : s + 1],
+                    in1=scores[:],
+                    op0=ALU.mult,
+                    op1=ALU.add,
+                )
+            return scores
+
+        def store_blocks(b, weights):
+            paired_ps = psum.tile([P, PAIR, TILES * BAND], F32, tag="block")
+            for e in range(PAIR):
+                nc.tensor.matmul(
+                    out=paired_ps[:, e, :],
+                    lhsT=pick[:, e, :],
+                    rhs=weights[:].rearrange("p n j -> p (n j)"),
+                    start=True,
+                    stop=True,
+                )
+            paired = work.tile([P, TILES, PAIR, BAND], F32)
+            nc.vector.tensor_copy(out=paired[:], in_=paired_ps[:].rearrange("p e (n j) -> p n e j", j=BAND))
+            nc.sync.dma_start(
+                out=out[b].rearrange("(n m e) j -> m n (e j)", m=P // PAIR, e=PAIR),
+                in_=paired[0 : P // PAIR].rearrange("m n e j -> m n (e j)"),
+            )
+
+        q_run = keep.tile([P, RUN, D], F32)
+        run_scores = keep.tile([P, RUN, BAND], F32)
+
+        def transpose_back(qT, i):
             for h in range(HALVES):
-                q = psum.tile([P, BANK], F32, tag="q", bufs=4)
-                for c in range(GROUP):
+                q_ps = psum.tile([P, BANK], F32, tag="xT")
+                for c in range(BANK // P):
                     nc.tensor.transpose(
-                        q[:, P * c : P * (c + 1)], qT[:, GROUP * h + c, P * m : P * (m + 1)], ident[:]
+                        q_ps[:, P * c : P * (c + 1)],
+                        qT[:, (BANK // P) * h + c, P * i : P * (i + 1)],
+                        ident[:],
                     )
-                for j in range(BAND):
-                    products = work.tile([P, BANK], F32, bufs=4)
-                    nc.vector.scalar_tensor_tensor(
-                        out=products[:],
-                        in0=q[:],
-                        scalar=1.0,
-                        in1=k_sb[:, i + j, BANK * h : BANK * (h + 1)],
-                        op0=ALU.mult,
-                        op1=ALU.mult,
-                        accum_out=sums[:, i, j, h : h + 1],
-                    )
+                nc.scalar.copy(out=q_run[:, i, BANK * h : BANK * (h + 1)], in_=q_ps[:])
 
-        staged = quantise_group(0)
-        for t in range(GROUPS):
-            qT = project_group(staged[0], staged[1])
-            if t + 1 < GROUPS:
-                staged = quantise_group(t + 1)
-            for m in range(GROUP):
-                band_scores(GROUP * t + m, qT, m)
+        def run_product(i, j):
+            products = work.tile([P, D], F32, bufs=3)
+            nc.vector.scalar_tensor_tensor(
+                out=products[:],
+                in0=q_run[:, i, :],
+                scalar=1.0,
+                in1=k_run[:, i + j, :],
+                op0=ALU.mult,
+                op1=ALU.mult,
+                accum_out=run_scores[:, i, j : j + 1],
+            )
 
-        scores = keep.tile([P, RUN, BAND], F32)
-        nc.vector.tensor_reduce(out=scores[:], in_=sums[:], axis=AXIS.X, op=ALU.add)
-        nc.vector.tensor_add(out=scores[:], in0=scores[:], in1=edge_mask[:])
-        top = keep.tile([P, RUN], F32)
-        nc.vector.tensor_reduce(out=top[:], in_=scores[:], axis=AXIS.X, op=ALU.max)
-        nc.vector.tensor_sub(
-            out=scores[:], in0=scores[:], in1=top[:].unsqueeze(2).to_broadcast([P, RUN, BAND])
-        )
-        weights = keep.tile([P, RUN, BAND], F32)
-        nc.scalar.activation(out=weights[:], in_=scores[:], func=ACT.Exp)
-        total = keep.tile([P, RUN], F32)
-        nc.vector.tensor_reduce(out=total[:], in_=weights[:], axis=AXIS.X, op=ALU.add)
-        nc.vector.reciprocal(out=total[:], in_=total[:])
-        nc.vector.tensor_mul(
-            out=weights[:], in0=weights[:], in1=total[:].unsqueeze(2).to_broadcast([P, RUN, BAND])
-        )
-        nc.sync.dma_start(out=out_runs, in_=weights[:].rearrange("p i j -> p (i j)"))
+        def finish_run():
+            weights = softmax_rows(run_scores, run_mask)
+            nc.sync.dma_start(
+                out=out[0].rearrange("(p i) j -> p (i j)", i=RUN), in_=weights[:].rearrange("p i j -> p (i j)")
+            )
+
+        run_codes, run_planes = quantise_batch(0)
+        codes, planes = quantise_batch(1)
+        qT_run = project_batch(run_codes, run_planes)
+        for i in range(RUN):
+            transpose_back(qT_run, i)
+        kT = new_keys()
+        for n in range(TILES):
+            transpose_keys(kT, 1, n)
+        qT = project_batch(codes, planes)
+        products_done = 0
+        for b in range(1, BATCHES):
+            if b + 1 < BATCHES:
+                codes, planes = quantise_batch(b + 1)
+                next_kT = new_keys()
+            for n in range(TILES):
+                band_block(qT, kT, n)
+                if b > 1 and n == 0:
+                    store_blocks(b - 1, weights)
+                if b + 1 < BATCHES:
+                    transpose_keys(next_kT, b + 1, n)
+                for unit in range(products_done, min(products_done + PRODUCTS_PER_BLOCK, RUN * BAND)):
+                    run_product(unit // BAND, unit % BAND)
+                    if unit == RUN * BAND - 1:
+                        finish_run()
+                products_done += PRODUCTS_PER_BLOCK
+            if b + 1 < BATCHES:
+                kT = next_kT
+                qT = project_batch(codes, planes)
+            weights = softmax_rows(band_scores(), block_mask)
+        store_blocks(BATCHES - 1, weights)

@@ -26,6 +26,7 @@ K_PASS = P * PACK
 PASSES = D // K_PASS
 CHUNKS = D // P
 BANK = 512
+PSUM_BANKS = 8
 HALVES = D // BANK
 PAD = 8
 WINDOW = P + 2 * NB
@@ -43,7 +44,7 @@ def tile_crosssliceattention_pa_kernel(tc, x, Wq_words, Wq_scales, bq, k_proj, o
     nc = tc.nc
 
     with tc.tile_pool(name="keep", bufs=1) as keep, tc.tile_pool(name="work", bufs=2) as work, tc.psum_pool(
-        name="psum", bufs=2
+        name="psum", bufs=PSUM_BANKS
     ) as psum:
         x_sb = keep.tile([P, BATCHES, TILES, D], BF16)
         k_run = keep.tile([P, SLOTS, D], BF16)
@@ -104,14 +105,6 @@ def tile_crosssliceattention_pa_kernel(tc, x, Wq_words, Wq_scales, bq, k_proj, o
         nc.vector.memset(warm[:], 0.0)
         nc.scalar.activation(out=warm[:], in_=warm[:], func=ACT.Exp)
 
-        bias_rows = keep.tile([P, P], F32)
-        nc.vector.memset(bias_rows[:], 0.0)
-        nc.vector.tensor_scalar_mul(out=bias_rows[0:CHUNKS, :], in0=bias_raw[:], scalar1=SCORE_SCALE)
-        bias_ps = psum.tile([P, P], F32, tag="xT")
-        nc.tensor.transpose(bias_ps[:], bias_rows[:], ident[:])
-        bias_col = keep.tile([P, CHUNKS], F32)
-        nc.vector.tensor_copy(out=bias_col[:], in_=bias_ps[:, 0:CHUNKS])
-
         pick = keep.tile([P, PAIR, P], F32)
         nc.vector.memset(pick[:], 0.0)
         nc.vector.tensor_copy(
@@ -162,7 +155,7 @@ def tile_crosssliceattention_pa_kernel(tc, x, Wq_words, Wq_scales, bq, k_proj, o
             grouped_pairs = grouped[:].bitcast(F32)
             for m in range(TILES):
                 x_pairs = x_sb[:, b, m, :].bitcast(F32)
-                xT = psum.tile([P, PASSES, 2, P], F32, tag="xT")
+                xT = psum.tile([P, PASSES, 2, P], F32, tag="bank")
                 for g in range(PASSES):
                     for u in range(2):
                         first = (K_PASS // 2) * g + u
@@ -185,7 +178,7 @@ def tile_crosssliceattention_pa_kernel(tc, x, Wq_words, Wq_scales, bq, k_proj, o
         def project_batch(codes, planes):
             qT = work.tile([P, CHUNKS, SEQ], F32)
             for c in range(CHUNKS):
-                acc = psum.tile([P, SEQ], F32, tag="acc")
+                acc = psum.tile([P, SEQ], F32, tag="bank")
                 for g in range(PASSES):
                     nc.tensor.matmul_mx(
                         out=acc[:],
@@ -212,14 +205,13 @@ def tile_crosssliceattention_pa_kernel(tc, x, Wq_words, Wq_scales, bq, k_proj, o
             return kT
 
         def transpose_keys(kT, b, n):
-            kT_ps = psum.tile([P, CHUNKS, P], BF16, tag="kT")
+            kT_ps = psum.tile([P, CHUNKS, P], BF16, tag="bank")
             for c in range(CHUNKS):
                 nc.tensor.transpose(kT_ps[:, c, :], k_sb[:, b - 1, n, P * c : P * (c + 1)], ident_bf[:])
             nc.scalar.copy(out=kT[:, :, PAD + P * n : PAD + P * (n + 1)], in_=kT_ps[:])
 
-        def softmax_rows(scores, mask):
+        def softmax_rows(scores):
             rows = [P, scores.shape[1]]
-            nc.vector.tensor_add(out=scores[:], in0=scores[:], in1=mask[:])
             top = work.tile(rows, F32)
             nc.vector.tensor_reduce(out=top[:], in_=scores[:], axis=AXIS.X, op=ALU.max)
             nc.vector.tensor_sub(
@@ -236,7 +228,7 @@ def tile_crosssliceattention_pa_kernel(tc, x, Wq_words, Wq_scales, bq, k_proj, o
             return weights
 
         def band_block(qT, kT, n):
-            block = psum.tile([P, WINDOW], F32, tag="block")
+            block = psum.tile([P, WINDOW], F32, tag="bank")
             first_key = PAD - NB + P * n
             for c in range(CHUNKS):
                 nc.tensor.matmul(
@@ -258,21 +250,25 @@ def tile_crosssliceattention_pa_kernel(tc, x, Wq_words, Wq_scales, bq, k_proj, o
             )
             nc.vector.tensor_copy(out=folded[:, :, 1, :], in_=folded[:, :, 0, :])
             twice = folded[:].rearrange("p n t r -> p n (t r)")
-            scores = work.tile([P, TILES, BAND], F32)
-            nc.vector.tensor_scalar_mul(out=scores[:], in0=twice[:, :, 0:BAND], scalar1=turn[:, 0:1])
+            windows = work.tile([P, TILES, BAND, BAND], F32)
+            nc.vector.scalar_tensor_tensor(
+                out=windows[:, :, :, 0],
+                in0=twice[:, :, 0:BAND],
+                scalar=turn[:, 0:1],
+                in1=block_mask[:],
+                op0=ALU.mult,
+                op1=ALU.add,
+            )
             for s in range(1, BAND):
-                nc.vector.scalar_tensor_tensor(
-                    out=scores[:],
-                    in0=twice[:, :, s : s + BAND],
-                    scalar=turn[:, s : s + 1],
-                    in1=scores[:],
-                    op0=ALU.mult,
-                    op1=ALU.add,
+                nc.vector.tensor_scalar_mul(
+                    out=windows[:, :, :, s], in0=twice[:, :, s : s + BAND], scalar1=turn[:, s : s + 1]
                 )
+            scores = work.tile([P, TILES, BAND], F32)
+            nc.vector.tensor_reduce(out=scores[:], in_=windows[:], axis=AXIS.X, op=ALU.add)
             return scores
 
         def store_blocks(b, weights):
-            paired_ps = psum.tile([P, PAIR, TILES * BAND], F32, tag="block")
+            paired_ps = psum.tile([P, PAIR, TILES * BAND], F32, tag="bank")
             for e in range(PAIR):
                 nc.tensor.matmul(
                     out=paired_ps[:, e, :],
@@ -293,14 +289,14 @@ def tile_crosssliceattention_pa_kernel(tc, x, Wq_words, Wq_scales, bq, k_proj, o
 
         def transpose_back(qT, i):
             for h in range(HALVES):
-                q_ps = psum.tile([P, BANK], F32, tag="xT")
+                q_ps = psum.tile([P, BANK], F32, tag="bank")
                 for c in range(BANK // P):
                     nc.tensor.transpose(
                         q_ps[:, P * c : P * (c + 1)],
                         qT[:, (BANK // P) * h + c, P * i : P * (i + 1)],
                         ident[:],
                     )
-                nc.scalar.copy(out=q_run[:, i, BANK * h : BANK * (h + 1)], in_=q_ps[:])
+                nc.vector.tensor_copy(out=q_run[:, i, BANK * h : BANK * (h + 1)], in_=q_ps[:])
 
         def run_product(i, j):
             products = work.tile([P, D], F32, bufs=3)
@@ -315,13 +311,23 @@ def tile_crosssliceattention_pa_kernel(tc, x, Wq_words, Wq_scales, bq, k_proj, o
             )
 
         def finish_run():
-            weights = softmax_rows(run_scores, run_mask)
+            nc.vector.tensor_add(out=run_scores[:], in0=run_scores[:], in1=run_mask[:])
+            weights = softmax_rows(run_scores)
             nc.sync.dma_start(
                 out=out[0].rearrange("(p i) j -> p (i j)", i=RUN), in_=weights[:].rearrange("p i j -> p (i j)")
             )
 
         run_codes, run_planes = quantise_batch(0)
         codes, planes = quantise_batch(1)
+
+        bias_rows = keep.tile([P, P], F32)
+        nc.vector.memset(bias_rows[:], 0.0)
+        nc.vector.tensor_scalar_mul(out=bias_rows[0:CHUNKS, :], in0=bias_raw[:], scalar1=SCORE_SCALE)
+        bias_ps = psum.tile([P, P], F32, tag="bank")
+        nc.tensor.transpose(bias_ps[:], bias_rows[:], ident[:])
+        bias_col = keep.tile([P, CHUNKS], F32)
+        nc.vector.tensor_copy(out=bias_col[:], in_=bias_ps[:, 0:CHUNKS])
+
         qT_run = project_batch(run_codes, run_planes)
         for i in range(RUN):
             transpose_back(qT_run, i)
@@ -348,5 +354,5 @@ def tile_crosssliceattention_pa_kernel(tc, x, Wq_words, Wq_scales, bq, k_proj, o
             if b + 1 < BATCHES:
                 kT = next_kT
                 qT = project_batch(codes, planes)
-            weights = softmax_rows(band_scores(), block_mask)
+            weights = softmax_rows(band_scores())
         store_blocks(BATCHES - 1, weights)

@@ -155,13 +155,14 @@ def tile_crosssliceattention_pa_kernel(tc, x, Wq_words, Wq_scales, bq, k_proj, o
             grouped_pairs = grouped[:].bitcast(F32)
             for m in range(TILES):
                 x_pairs = x_sb[:, b, m, :].bitcast(F32)
+                sorted_pairs = work.tile([P, PASSES, 2, P], F32, bufs=3)
+                nc.vector.tensor_copy(
+                    out=sorted_pairs[:], in_=x_pairs.rearrange("p (g q u) -> p g u q", g=PASSES, u=2)
+                )
                 xT = psum.tile([P, PASSES, 2, P], F32, tag="bank")
                 for g in range(PASSES):
                     for u in range(2):
-                        first = (K_PASS // 2) * g + u
-                        nc.tensor.transpose(
-                            xT[:, g, u, :], x_pairs[:, first : (K_PASS // 2) * (g + 1) : 2], ident[:]
-                        )
+                        nc.tensor.transpose(xT[:, g, u, :], sorted_pairs[:, g, u, :], ident[:])
                 nc.scalar.copy(
                     out=grouped_pairs[:, :, P * m : P * (m + 1), :],
                     in_=xT[:].rearrange("p g u m -> p g m u"),

@@ -155,14 +155,13 @@ def tile_crosssliceattention_pa_kernel(tc, x, Wq_words, Wq_scales, bq, k_proj, o
             grouped_pairs = grouped[:].bitcast(F32)
             for m in range(TILES):
                 x_pairs = x_sb[:, b, m, :].bitcast(F32)
-                sorted_pairs = work.tile([P, PASSES, 2, P], F32, bufs=3)
-                nc.vector.tensor_copy(
-                    out=sorted_pairs[:], in_=x_pairs.rearrange("p (g q u) -> p g u q", g=PASSES, u=2)
-                )
                 xT = psum.tile([P, PASSES, 2, P], F32, tag="bank")
                 for g in range(PASSES):
                     for u in range(2):
-                        nc.tensor.transpose(xT[:, g, u, :], sorted_pairs[:, g, u, :], ident[:])
+                        first = (K_PASS // 2) * g + u
+                        nc.tensor.transpose(
+                            xT[:, g, u, :], x_pairs[:, first : (K_PASS // 2) * (g + 1) : 2], ident[:]
+                        )
                 nc.scalar.copy(
                     out=grouped_pairs[:, :, P * m : P * (m + 1), :],
                     in_=xT[:].rearrange("p g u m -> p g m u"),
@@ -288,16 +287,29 @@ def tile_crosssliceattention_pa_kernel(tc, x, Wq_words, Wq_scales, bq, k_proj, o
         q_run = keep.tile([P, RUN, D], F32)
         run_scores = keep.tile([P, RUN, BAND], F32)
 
-        def transpose_back(qT, i):
-            for h in range(HALVES):
-                q_ps = psum.tile([P, BANK], F32, tag="bank")
-                for c in range(BANK // P):
-                    nc.tensor.transpose(
-                        q_ps[:, P * c : P * (c + 1)],
-                        qT[:, (BANK // P) * h + c, P * i : P * (i + 1)],
-                        ident[:],
+        def project_run(codes, planes):
+            for i in range(RUN):
+                for h in range(HALVES):
+                    features = slice(BANK * h, BANK * (h + 1))
+                    acc = psum.tile([P, BANK], F32, tag="bank")
+                    for g in range(PASSES):
+                        nc.tensor.matmul_mx(
+                            out=acc[:],
+                            lhsT=codes[:, g, P * i : P * (i + 1)].bitcast(FP8X4),
+                            lhsT_scale=planes[:, g, P * i : P * (i + 1)],
+                            rhs=w_words[:, g, 2 * BANK * h : 2 * BANK * (h + 1)].bitcast(FP4X4),
+                            rhs_scale=w_planes[:, g, features],
+                            start=(g == 0),
+                            stop=(g == PASSES - 1),
+                        )
+                    nc.vector.scalar_tensor_tensor(
+                        out=q_run[:, i, features],
+                        in0=acc[:],
+                        scalar=SCORE_SCALE,
+                        in1=bias_wide[:, features],
+                        op0=ALU.mult,
+                        op1=ALU.add,
                     )
-                nc.vector.tensor_copy(out=q_run[:, i, BANK * h : BANK * (h + 1)], in_=q_ps[:])
 
         def run_product(i, j):
             products = work.tile([P, D], F32, bufs=3)
@@ -328,10 +340,17 @@ def tile_crosssliceattention_pa_kernel(tc, x, Wq_words, Wq_scales, bq, k_proj, o
         nc.tensor.transpose(bias_ps[:], bias_rows[:], ident[:])
         bias_col = keep.tile([P, CHUNKS], F32)
         nc.vector.tensor_copy(out=bias_col[:], in_=bias_ps[:, 0:CHUNKS])
+        bias_wide = keep.tile([P, D], F32)
+        for h in range(HALVES):
+            wide_ps = psum.tile([P, BANK], F32, tag="bank")
+            for c in range(BANK // P):
+                chunk = (BANK // P) * h + c
+                nc.tensor.transpose(
+                    wide_ps[:, P * c : P * (c + 1)], bias_col[:, chunk : chunk + 1].to_broadcast([P, P]), ident[:]
+                )
+            nc.vector.tensor_copy(out=bias_wide[:, BANK * h : BANK * (h + 1)], in_=wide_ps[:])
 
-        qT_run = project_batch(run_codes, run_planes)
-        for i in range(RUN):
-            transpose_back(qT_run, i)
+        project_run(run_codes, run_planes)
         kT = new_keys()
         for n in range(TILES):
             transpose_keys(kT, 1, n)

@@ -19,7 +19,8 @@ BATCHES, SEQ, D = 4, 512, 1024
 NB = 2
 BAND = 2 * NB + 1
 TILES = SEQ // P
-RUN = SEQ // P
+BLOCKS = BATCHES * TILES
+RUN = 6
 SLOTS = RUN + 2 * NB
 PACK = 4
 K_PASS = P * PACK
@@ -31,288 +32,249 @@ HALVES = D // BANK
 PAD = 8
 WINDOW = P + 2 * NB
 FOLDS = -(-WINDOW // BAND)
+REPEATS = BAND + 1
 PAIR = 2
 SCORE_SCALE = 1.0 / math.sqrt(D)
 MASKED = -1.0e30
 HALO_CUT = 112
-PRODUCTS_PER_BLOCK = 2
+SORT_BUFS = 8
+SORT_ENGINE = "vector"
+PRODUCTS_HEAD = 8
+PRODUCTS_PER_BLOCK = 3
+LAST_ALONE = False
+LINKS_PER_BLOCK = 2
+EVEN_ENGINE = "scalar"
 
 FLOPS = 2 * BATCHES * SEQ * D * D + 2 * BATCHES * SEQ * BAND * D
 
 
 def tile_crosssliceattention_pa_kernel(tc, x, Wq_words, Wq_scales, bq, k_proj, out):
     nc = tc.nc
+    x_rows = x.rearrange("b s k -> (b s) k")
+    k_rows = k_proj.rearrange("b s d -> (b s) d")
+    out_rows = out.rearrange("b s j -> (b s) j")
+    groups = [(max(TILES * b, RUN), TILES * (b + 1) - max(TILES * b, RUN)) for b in range(BATCHES) if TILES * (b + 1) > RUN]
+    halo_block = RUN % TILES != 0
 
     with tc.tile_pool(name="keep", bufs=1) as keep, tc.tile_pool(name="work", bufs=2) as work, tc.psum_pool(
         name="psum", bufs=PSUM_BANKS
     ) as psum:
-        x_sb = keep.tile([P, BATCHES, TILES, D], BF16)
+        x_run = keep.tile([P, RUN, D], BF16)
+        x_sb = keep.tile([P, BLOCKS - RUN, D], BF16)
         k_run = keep.tile([P, SLOTS, D], BF16)
-        k_sb = keep.tile([P, BATCHES - 1, TILES, D], BF16)
+        k_sb = keep.tile([P, BLOCKS - RUN + 1, D], BF16)
         w_words = keep.tile([P, PASSES, 2 * D], U8, align_bytes=64)
         w_planes = keep.tile([P, PASSES, D], U8, align_bytes=64)
         bias_raw = keep.tile([CHUNKS, P], BF16)
 
         nc.vector.memset(w_planes[:].bitcast(I32), 0)
-        nc.vector.memset(k_run[0:1, 0:NB, :], 0.0)
-        nc.vector.memset(k_run[P - 32 : P, SLOTS - NB : SLOTS, :], 0.0)
 
-        def load_x(b):
-            if b == 0:
-                tiles = x[b].rearrange("(p i) k -> p i k", i=RUN)
-            else:
-                tiles = x[b].rearrange("(n p) k -> p n k", p=P)
-            for m in range(TILES):
-                nc.sync.dma_start(out=x_sb[:, b, m, :], in_=tiles[:, m, :])
+        def load_x_run(i):
+            nc.sync.dma_start(out=x_run[:, i, :], in_=x_rows[0 : P * RUN].rearrange("(p i) k -> p i k", i=RUN)[:, i, :])
 
-        def load_k(b):
-            nc.sync.dma_start(out=k_sb[:, b - 1, :, :], in_=k_proj[b].rearrange("(n p) d -> p n d", p=P))
+        def load_x(t):
+            nc.sync.dma_start(out=x_sb[:, t - RUN, :], in_=x_rows[P * t : P * (t + 1)])
 
-        def load_k_run():
-            runs = k_proj[0].rearrange("(p i) d -> p i d", i=RUN)
-            nc.sync.dma_start(out=k_run[:, NB : NB + RUN, :], in_=runs)
-            cut = P - HALO_CUT
-            nc.sync.dma_start(out=k_run[1:cut, 0:NB, :], in_=runs[0 : cut - 1, RUN - NB : RUN, :])
-            nc.sync.dma_start(out=k_run[cut:P, 0:NB, :], in_=runs[cut - 1 : P - 1, RUN - NB : RUN, :])
-            nc.sync.dma_start(out=k_run[0:HALO_CUT, SLOTS - NB : SLOTS, :], in_=runs[1 : HALO_CUT + 1, 0:NB, :])
+        def load_k(first, blocks):
             nc.sync.dma_start(
-                out=k_run[HALO_CUT : P - 1, SLOTS - NB : SLOTS, :], in_=runs[HALO_CUT + 1 : P, 0:NB, :]
+                out=k_sb[:, first - RUN + 1 : first - RUN + 1 + blocks, :],
+                in_=k_rows[P * first : P * (first + blocks)].rearrange("(n p) d -> p n d", p=P),
             )
+
+        def load_w(h):
+            half = slice(2 * BANK * h, 2 * BANK * (h + 1))
+            nc.sync.dma_start(
+                out=w_words[:, :, half].bitcast(I32),
+                in_=Wq_words.rearrange("g p b -> p g b")[:, :, half].bitcast(I32),
+            )
+
+        def load_scales():
+            for quad in range(4):
+                nc.sync.dma_start(
+                    out=w_planes[32 * quad : 32 * quad + 4].bitcast(I32),
+                    in_=Wq_scales[:, 4 * quad : 4 * quad + 4, :].rearrange("g r n -> r g n").bitcast(I32),
+                )
+
+        def load_k_run_own(first, last):
+            nc.sync.dma_start(
+                out=k_run[:, NB + first : NB + last, :],
+                in_=k_rows[0 : P * RUN].rearrange("(p i) d -> p i d", i=RUN)[:, first:last, :],
+            )
+
+        def load_k_run_left():
+            before = k_rows[RUN - NB : RUN - NB + (P - 1) * RUN].rearrange("(p i) d -> p i d", i=RUN)
+            cut = P - HALO_CUT
+            nc.sync.dma_start(out=k_run[1:cut, 0:NB, :], in_=before[0 : cut - 1, 0:NB, :])
+            nc.sync.dma_start(out=k_run[cut:P, 0:NB, :], in_=before[cut - 1 : P - 1, 0:NB, :])
+
+        def load_k_run_right():
+            after = k_rows[RUN : RUN + P * RUN].rearrange("(p i) d -> p i d", i=RUN)
+            nc.sync.dma_start(out=k_run[:, SLOTS - NB : SLOTS, :], in_=after[:, 0:NB, :])
 
         nc.sync.dma_start(out=bias_raw[:], in_=bq.rearrange("(c f) -> c f", f=P))
-        load_x(0)
-        load_x(1)
-        nc.sync.dma_start(
-            out=w_words[:].bitcast(I32), in_=Wq_words.rearrange("g p b -> p g b").bitcast(I32)
-        )
-        for quad in range(4):
-            nc.sync.dma_start(
-                out=w_planes[32 * quad : 32 * quad + 4].bitcast(I32),
-                in_=Wq_scales[:, 4 * quad : 4 * quad + 4, :].rearrange("g r n -> r g n").bitcast(I32),
-            )
-        load_k(1)
-        load_k_run()
-        for b in range(2, BATCHES):
-            load_x(b)
-            load_k(b)
+        load_x_run(0)
+        load_x_run(1)
+        load_scales()
+        load_w(0)
+        for i in range(2, RUN):
+            load_x_run(i)
+        load_w(1)
+        for index, (first, blocks) in enumerate(groups):
+            for m in range(blocks):
+                load_x(first + m)
+            if index == 0 and halo_block:
+                load_k(first - 1, blocks + 1)
+            else:
+                load_k(first, blocks)
+            if index == 0:
+                load_k_run_left()
+                load_k_run_own(0, RUN)
+                load_k_run_right()
 
         ident = keep.tile([P, P], F32)
-        make_identity(nc, ident[:])
         ident_bf = keep.tile([P, P], BF16)
-        make_identity(nc, ident_bf[:])
-
         warm = keep.tile([P, 1], F32)
-        nc.vector.memset(warm[:], 0.0)
-        nc.scalar.activation(out=warm[:], in_=warm[:], func=ACT.Exp)
-
         pick = keep.tile([P, PAIR, P], F32)
-        nc.vector.memset(pick[:], 0.0)
-        nc.vector.tensor_copy(
-            out=pick[:, :, 0 : P // PAIR], in_=ident[:].rearrange("p (m e) -> p e m", e=PAIR)
-        )
-
         run_mask = keep.tile([P, RUN, BAND], F32)
-        block_mask = keep.tile([P, TILES, BAND], F32)
-        nc.vector.memset(run_mask[:], 0.0)
-        nc.vector.memset(block_mask[:], 0.0)
-        for i in range(NB):
-            missing = NB - i
-            nc.vector.tensor_scalar_mul(
-                out=run_mask[:, i, 0:missing], in0=ident[:, 0:1].to_broadcast([P, missing]), scalar1=MASKED
-            )
-            nc.vector.tensor_scalar_mul(
-                out=run_mask[:, RUN - 1 - i, BAND - missing : BAND],
-                in0=ident[:, P - 1 : P].to_broadcast([P, missing]),
-                scalar1=MASKED,
-            )
-            for columns, partition in (
-                (block_mask[:, 0, 0:missing], i),
-                (block_mask[:, TILES - 1, BAND - missing : BAND], P - 1 - i),
-            ):
-                nc.vector.scalar_tensor_tensor(
-                    out=columns,
-                    in0=ident[:, partition : partition + 1].to_broadcast([P, missing]),
-                    scalar=MASKED,
-                    in1=columns,
-                    op0=ALU.mult,
-                    op1=ALU.add,
-                )
-
         in_band = keep.tile([P, WINDOW], F32)
-        nc.vector.memset(in_band[:], 0.0)
-        for j in range(BAND):
-            nc.vector.tensor_add(out=in_band[:, j : j + P], in0=in_band[:, j : j + P], in1=ident[:])
-        banded = keep.tile([P, TILES, FOLDS * BAND], F32)
-        nc.vector.memset(banded[:], 0.0)
+        banded = keep.tile([P, 2, TILES, (FOLDS + 1) * BAND], F32)
         turn = keep.tile([P, BAND], F32)
-        nc.vector.tensor_copy(out=banded[:, 0, 0:P], in_=ident[:])
-        nc.vector.tensor_reduce(
-            out=turn[:], in_=banded[:, 0, :].rearrange("p (a r) -> p r a", r=BAND), axis=AXIS.X, op=ALU.add
-        )
+        bias_rows = keep.tile([P, P], F32)
+        bias_col = keep.tile([P, CHUNKS], F32)
+        bias_wide = keep.tile([P, D], F32)
 
-        def quantise_batch(b):
-            grouped = work.tile([P, PASSES, SEQ, PACK], BF16, align_bytes=64)
-            grouped_pairs = grouped[:].bitcast(F32)
-            for m in range(TILES):
-                x_pairs = x_sb[:, b, m, :].bitcast(F32)
-                xT = psum.tile([P, PASSES, 2, P], F32, tag="bank")
-                for g in range(PASSES):
-                    for u in range(2):
-                        first = (K_PASS // 2) * g + u
-                        nc.tensor.transpose(
-                            xT[:, g, u, :], x_pairs[:, first : (K_PASS // 2) * (g + 1) : 2], ident[:]
-                        )
-                nc.scalar.copy(
-                    out=grouped_pairs[:, :, P * m : P * (m + 1), :],
-                    in_=xT[:].rearrange("p g u m -> p g m u"),
+        def setup_gpsimd():
+            make_identity(nc, ident[:])
+            nc.gpsimd.memset(bias_rows[:], 0.0)
+            nc.gpsimd.memset(warm[:], 0.0)
+            nc.scalar.activation(out=warm[:], in_=warm[:], func=ACT.Exp)
+            nc.gpsimd.memset(k_run[0:1, 0:NB, :], 0.0)
+            make_identity(nc, ident_bf[:])
+            nc.gpsimd.memset(run_mask[:], 0.0)
+            nc.gpsimd.memset(in_band[:], 0.0)
+            nc.gpsimd.memset(banded[:], 0.0)
+            nc.gpsimd.memset(pick[:], 0.0)
+            for j in range(BAND):
+                nc.gpsimd.tensor_tensor(
+                    out=in_band[:, j : j + P], in0=in_band[:, j : j + P], in1=ident[:], op=ALU.subtract
                 )
-            codes = work.tile([P, PASSES, SEQ], U32, align_bytes=64)
-            planes = work.tile([P, PASSES, SEQ], U8, align_bytes=64)
-            nc.vector.quantize_mx(
-                out=codes[:].rearrange("p g m -> p (g m)").bitcast(FP8X4),
-                scales=planes[:].rearrange("p g m -> p (g m)"),
-                in_=grouped[:].rearrange("p g m t -> p (g m t)"),
+            nc.gpsimd.tensor_copy(out=pick[:, :, 0 : P // PAIR], in_=ident[:].rearrange("p (m e) -> p e m", e=PAIR))
+            nc.gpsimd.tensor_scalar(
+                out=banded[:, 0, 0, 0:P], in0=ident[:], scalar1=float(REPEATS), scalar2=0.0, op0=ALU.mult, op1=ALU.add
             )
-            return codes, planes
 
-        def project_batch(codes, planes):
-            qT = work.tile([P, CHUNKS, SEQ], F32)
-            for c in range(CHUNKS):
-                acc = psum.tile([P, SEQ], F32, tag="bank")
-                for g in range(PASSES):
-                    nc.tensor.matmul_mx(
-                        out=acc[:],
-                        lhsT=w_words[:, g, 2 * P * c : 2 * P * (c + 1)].bitcast(FP4X4),
-                        lhsT_scale=w_planes[:, g, P * c : P * (c + 1)],
-                        rhs=codes[:, g, :].bitcast(FP8X4),
-                        rhs_scale=planes[:, g, :],
-                        start=(g == 0),
-                        stop=(g == PASSES - 1),
-                    )
-                nc.scalar.activation(
-                    out=qT[:, c, :],
-                    in_=acc[:],
-                    func=ACT.Identity,
-                    bias=bias_col[:, c : c + 1],
-                    scale=SCORE_SCALE,
-                )
-            return qT
-
-        def new_keys():
-            kT = work.tile([P, CHUNKS, PAD + SEQ + PAD], F32)
-            nc.gpsimd.memset(kT[:, :, 0:PAD], 0.0)
-            nc.gpsimd.memset(kT[:, :, PAD + SEQ : PAD + SEQ + PAD], 0.0)
-            return kT
-
-        def transpose_keys(kT, b, n):
-            kT_ps = psum.tile([P, CHUNKS, P], BF16, tag="bank")
-            for c in range(CHUNKS):
-                nc.tensor.transpose(kT_ps[:, c, :], k_sb[:, b - 1, n, P * c : P * (c + 1)], ident_bf[:])
-            nc.scalar.copy(out=kT[:, :, PAD + P * n : PAD + P * (n + 1)], in_=kT_ps[:])
-
-        def softmax_rows(scores):
-            rows = [P, scores.shape[1]]
-            top = work.tile(rows, F32)
-            nc.vector.tensor_reduce(out=top[:], in_=scores[:], axis=AXIS.X, op=ALU.max)
-            nc.vector.tensor_sub(
-                out=scores[:], in0=scores[:], in1=top[:].unsqueeze(2).to_broadcast(rows + [BAND])
-            )
-            weights = work.tile(rows + [BAND], F32)
-            nc.scalar.activation(out=weights[:], in_=scores[:], func=ACT.Exp)
-            total = work.tile(rows, F32)
-            nc.vector.tensor_reduce(out=total[:], in_=weights[:], axis=AXIS.X, op=ALU.add)
-            nc.vector.reciprocal(out=total[:], in_=total[:])
-            nc.vector.tensor_mul(
-                out=weights[:], in0=weights[:], in1=total[:].unsqueeze(2).to_broadcast(rows + [BAND])
-            )
-            return weights
-
-        def band_block(qT, kT, n):
-            block = psum.tile([P, WINDOW], F32, tag="bank")
-            first_key = PAD - NB + P * n
-            for c in range(CHUNKS):
-                nc.tensor.matmul(
-                    out=block[:],
-                    lhsT=qT[:, c, P * n : P * (n + 1)],
-                    rhs=kT[:, c, first_key : first_key + WINDOW],
-                    start=(c == 0),
-                    stop=(c == CHUNKS - 1),
-                )
-            nc.vector.tensor_mul(out=banded[:, n, 0:WINDOW], in0=block[:], in1=in_band[:])
-
-        def band_scores():
-            folded = work.tile([P, TILES, 2, BAND], F32)
+        def setup_band():
             nc.vector.tensor_reduce(
-                out=folded[:, :, 0, :],
-                in_=banded[:].rearrange("p n (a r) -> p n r a", r=BAND),
-                axis=AXIS.X,
-                op=ALU.add,
+                out=turn[:], in_=banded[:, 0, 0, :].rearrange("p (a r) -> p r a", r=BAND), axis=AXIS.X, op=ALU.add
             )
-            nc.vector.tensor_copy(out=folded[:, :, 1, :], in_=folded[:, :, 0, :])
-            twice = folded[:].rearrange("p n t r -> p n (t r)")
-            windows = work.tile([P, TILES, BAND, BAND], F32)
-            nc.vector.scalar_tensor_tensor(
-                out=windows[:, :, :, 0],
-                in0=twice[:, :, 0:BAND],
-                scalar=turn[:, 0:1],
-                in1=block_mask[:],
-                op0=ALU.mult,
-                op1=ALU.add,
-            )
-            for s in range(1, BAND):
-                nc.vector.tensor_scalar_mul(
-                    out=windows[:, :, :, s], in0=twice[:, :, s : s + BAND], scalar1=turn[:, s : s + 1]
-                )
-            scores = work.tile([P, TILES, BAND], F32)
-            nc.vector.tensor_reduce(out=scores[:], in_=windows[:], axis=AXIS.X, op=ALU.add)
-            return scores
-
-        def store_blocks(b, weights):
-            paired_ps = psum.tile([P, PAIR, TILES * BAND], F32, tag="bank")
-            for e in range(PAIR):
-                nc.tensor.matmul(
-                    out=paired_ps[:, e, :],
-                    lhsT=pick[:, e, :],
-                    rhs=weights[:].rearrange("p n j -> p (n j)"),
-                    start=True,
-                    stop=True,
-                )
-            paired = work.tile([P, TILES, PAIR, BAND], F32)
-            nc.vector.tensor_copy(out=paired[:], in_=paired_ps[:].rearrange("p e (n j) -> p n e j", j=BAND))
-            nc.sync.dma_start(
-                out=out[b].rearrange("(n m e) j -> m n (e j)", m=P // PAIR, e=PAIR),
-                in_=paired[0 : P // PAIR].rearrange("m n e j -> m n (e j)"),
-            )
-
-        q_run = keep.tile([P, RUN, D], F32)
-        run_scores = keep.tile([P, RUN, BAND], F32)
-
-        def project_run(codes, planes):
-            for i in range(RUN):
-                for h in range(HALVES):
-                    features = slice(BANK * h, BANK * (h + 1))
-                    acc = psum.tile([P, BANK], F32, tag="bank")
-                    for g in range(PASSES):
-                        nc.tensor.matmul_mx(
-                            out=acc[:],
-                            lhsT=codes[:, g, P * i : P * (i + 1)].bitcast(FP8X4),
-                            lhsT_scale=planes[:, g, P * i : P * (i + 1)],
-                            rhs=w_words[:, g, 2 * BANK * h : 2 * BANK * (h + 1)].bitcast(FP4X4),
-                            rhs_scale=w_planes[:, g, features],
-                            start=(g == 0),
-                            stop=(g == PASSES - 1),
+            for i in range(NB):
+                for t in range(NB - i):
+                    for n, m, w in ((0, i, i + t), (TILES - 1, P - 1 - i, P - 1 - i + BAND - 1 - t)):
+                        place = FOLDS * BAND + w % BAND
+                        nc.vector.scalar_tensor_tensor(
+                            out=banded[:, :, n, place],
+                            in0=ident[:, m : m + 1].to_broadcast([P, 2]),
+                            scalar=-MASKED,
+                            in1=banded[:, :, n, place],
+                            op0=ALU.mult,
+                            op1=ALU.add,
                         )
+
+        def setup_run_mask():
+            for t in range(P * RUN):
+                s = t % SEQ
+                missing = max(NB - s, NB - (SEQ - 1 - s))
+                if missing > 0:
+                    first = 0 if s < NB else BAND - missing
+                    columns = run_mask[:, t % RUN, first : first + missing]
                     nc.vector.scalar_tensor_tensor(
-                        out=q_run[:, i, features],
-                        in0=acc[:],
-                        scalar=SCORE_SCALE,
-                        in1=bias_wide[:, features],
+                        out=columns,
+                        in0=ident[:, t // RUN : t // RUN + 1].to_broadcast([P, missing]),
+                        scalar=MASKED,
+                        in1=columns,
                         op0=ALU.mult,
                         op1=ALU.add,
                     )
 
+        def bias_column():
+            nc.vector.tensor_scalar_mul(out=bias_rows[0:CHUNKS, :], in0=bias_raw[:], scalar1=SCORE_SCALE)
+            bias_ps = psum.tile([P, P], F32, tag="bank")
+            nc.tensor.transpose(bias_ps[:], bias_rows[:], ident[:])
+            nc.vector.tensor_copy(out=bias_col[:], in_=bias_ps[:, 0:CHUNKS])
+
+        def bias_row(h):
+            wide_ps = psum.tile([P, BANK], F32, tag="bank")
+            for c in range(BANK // P):
+                chunk = (BANK // P) * h + c
+                nc.tensor.transpose(
+                    wide_ps[:, P * c : P * (c + 1)], bias_col[:, chunk : chunk + 1].to_broadcast([P, P]), ident[:]
+                )
+            nc.vector.tensor_copy(out=bias_wide[:, BANK * h : BANK * (h + 1)], in_=wide_ps[:])
+
+        def copy_out(engine, out_ap, in_ap):
+            if engine == "scalar":
+                nc.scalar.copy(out=out_ap, in_=in_ap)
+            else:
+                nc.vector.tensor_copy(out=out_ap, in_=in_ap)
+
+        def transpose_words(tokens, sort):
+            x_pairs = tokens.bitcast(F32)
+            xT = psum.tile([P, PASSES, 2, P], F32, tag="bank")
+            for g in range(PASSES):
+                for u in range(2):
+                    first = (K_PASS // 2) * g + u
+                    if sort is None:
+                        nc.tensor.transpose(xT[:, g, u, :], x_pairs[:, first : (K_PASS // 2) * (g + 1) : 2], ident[:])
+                    else:
+                        nc.tensor.transpose(xT[:, g, u, :], sort[:, g, u, :], ident[:])
+            return xT
+
+        def sort_words(tokens, engine):
+            x_sorted = work.tile([P, PASSES, 2, P], F32, bufs=SORT_BUFS)
+            copy_out(engine, x_sorted[:], tokens.bitcast(F32).rearrange("t (g p u) -> t g u p", g=PASSES, u=2))
+            return x_sorted
+
+        q_run = keep.tile([P, RUN, D], F32)
+        run_scores = keep.tile([P, RUN, BAND], F32)
+        run_grouped = keep.tile([P, RUN, PASSES, P, PACK], BF16, align_bytes=64)
+        run_codes = keep.tile([P, RUN, PASSES, P], U32, align_bytes=64)
+        run_planes = keep.tile([P, RUN, PASSES, P], U8, align_bytes=64)
+
+        def run_transpose(i, engine="scalar", sort=None):
+            xT = transpose_words(x_run[:, i, :], sort)
+            copy_out(engine, run_grouped[:].bitcast(F32)[:, i], xT[:].rearrange("p g u m -> p g m u"))
+
+        def run_quantise(i):
+            nc.vector.quantize_mx(
+                out=run_codes[:, i].rearrange("p g m -> p (g m)").bitcast(FP8X4),
+                scales=run_planes[:, i].rearrange("p g m -> p (g m)"),
+                in_=run_grouped[:, i].rearrange("p g m t -> p (g m t)"),
+            )
+
+        def run_project(i, h):
+            features = slice(BANK * h, BANK * (h + 1))
+            acc = psum.tile([P, BANK], F32, tag="bank")
+            for g in range(PASSES):
+                nc.tensor.matmul_mx(
+                    out=acc[:],
+                    lhsT=run_codes[:, i, g, :].bitcast(FP8X4),
+                    lhsT_scale=run_planes[:, i, g, :],
+                    rhs=w_words[:, g, 2 * BANK * h : 2 * BANK * (h + 1)].bitcast(FP4X4),
+                    rhs_scale=w_planes[:, g, features],
+                    start=(g == 0),
+                    stop=(g == PASSES - 1),
+                )
+            nc.vector.scalar_tensor_tensor(
+                out=q_run[:, i, features],
+                in0=acc[:],
+                scalar=SCORE_SCALE,
+                in1=bias_wide[:, features],
+                op0=ALU.mult,
+                op1=ALU.add,
+            )
+
         def run_product(i, j):
-            products = work.tile([P, D], F32, bufs=3)
+            products = work.tile([P, D], F32, bufs=2)
             nc.vector.scalar_tensor_tensor(
                 out=products[:],
                 in0=q_run[:, i, :],
@@ -323,56 +285,303 @@ def tile_crosssliceattention_pa_kernel(tc, x, Wq_words, Wq_scales, bq, k_proj, o
                 accum_out=run_scores[:, i, j : j + 1],
             )
 
-        def finish_run():
-            nc.vector.tensor_add(out=run_scores[:], in0=run_scores[:], in1=run_mask[:])
-            weights = softmax_rows(run_scores)
-            nc.sync.dma_start(
-                out=out[0].rearrange("(p i) j -> p (i j)", i=RUN), in_=weights[:].rearrange("p i j -> p (i j)")
-            )
+        def run_chain():
+            rows = [P, RUN]
+            top = work.tile(rows, F32)
+            run_weights = work.tile(rows + [BAND], F32)
+            run_total = work.tile(rows, F32)
 
-        run_codes, run_planes = quantise_batch(0)
-        codes, planes = quantise_batch(1)
-
-        bias_rows = keep.tile([P, P], F32)
-        nc.vector.memset(bias_rows[:], 0.0)
-        nc.vector.tensor_scalar_mul(out=bias_rows[0:CHUNKS, :], in0=bias_raw[:], scalar1=SCORE_SCALE)
-        bias_ps = psum.tile([P, P], F32, tag="bank")
-        nc.tensor.transpose(bias_ps[:], bias_rows[:], ident[:])
-        bias_col = keep.tile([P, CHUNKS], F32)
-        nc.vector.tensor_copy(out=bias_col[:], in_=bias_ps[:, 0:CHUNKS])
-        bias_wide = keep.tile([P, D], F32)
-        for h in range(HALVES):
-            wide_ps = psum.tile([P, BANK], F32, tag="bank")
-            for c in range(BANK // P):
-                chunk = (BANK // P) * h + c
-                nc.tensor.transpose(
-                    wide_ps[:, P * c : P * (c + 1)], bias_col[:, chunk : chunk + 1].to_broadcast([P, P]), ident[:]
+            def shift():
+                nc.vector.tensor_add(out=run_scores[:], in0=run_scores[:], in1=run_mask[:])
+                nc.vector.tensor_reduce(out=top[:], in_=run_scores[:], axis=AXIS.X, op=ALU.max)
+                nc.vector.tensor_sub(
+                    out=run_scores[:], in0=run_scores[:], in1=top[:].unsqueeze(2).to_broadcast(rows + [BAND])
                 )
-            nc.vector.tensor_copy(out=bias_wide[:, BANK * h : BANK * (h + 1)], in_=wide_ps[:])
 
-        project_run(run_codes, run_planes)
-        kT = new_keys()
-        for n in range(TILES):
-            transpose_keys(kT, 1, n)
-        qT = project_batch(codes, planes)
-        products_done = 0
-        for b in range(1, BATCHES):
-            if b + 1 < BATCHES:
-                codes, planes = quantise_batch(b + 1)
-                next_kT = new_keys()
-            for n in range(TILES):
-                band_block(qT, kT, n)
-                if b > 1 and n == 0:
-                    store_blocks(b - 1, weights)
-                if b + 1 < BATCHES:
-                    transpose_keys(next_kT, b + 1, n)
-                for unit in range(products_done, min(products_done + PRODUCTS_PER_BLOCK, RUN * BAND)):
-                    run_product(unit // BAND, unit % BAND)
-                    if unit == RUN * BAND - 1:
-                        finish_run()
-                products_done += PRODUCTS_PER_BLOCK
-            if b + 1 < BATCHES:
+            def exps():
+                nc.scalar.activation(out=run_weights[:], in_=run_scores[:], func=ACT.Exp)
+
+            def divide():
+                nc.vector.tensor_reduce(out=run_total[:], in_=run_weights[:], axis=AXIS.X, op=ALU.add)
+                nc.vector.reciprocal(out=run_total[:], in_=run_total[:])
+                nc.vector.tensor_mul(
+                    out=run_weights[:], in0=run_weights[:], in1=run_total[:].unsqueeze(2).to_broadcast(rows + [BAND])
+                )
+                nc.sync.dma_start(
+                    out=out_rows[0 : P * RUN].rearrange("(p i) j -> p (i j)", i=RUN),
+                    in_=run_weights[:].rearrange("p i j -> p (i j)"),
+                )
+
+            return [shift, exps, divide]
+
+        def new_x():
+            grouped = work.tile([P, PASSES, SEQ, PACK], BF16, align_bytes=64)
+            return grouped
+
+        def transpose_x(grouped, first, blocks, m, engine="scalar", sort=None):
+            xT = transpose_words(x_sb[:, first + m - RUN, :], sort)
+            pairs = grouped[:].bitcast(F32)
+            if blocks == TILES:
+                copy_out(engine, pairs[:, :, P * m : P * (m + 1), :], xT[:].rearrange("p g u m -> p g m u"))
+            else:
+                by_block = grouped[:].rearrange("p g m t -> p (g m t)").bitcast(F32).rearrange(
+                    "p (n g m u) -> p n g m u", g=PASSES, m=P, u=2
+                )
+                copy_out(engine, by_block[:, m], xT[:].rearrange("p g u m -> p g m u"))
+
+        def new_codes():
+            codes = work.tile([P, PASSES, SEQ], U32, align_bytes=64)
+            planes = work.tile([P, PASSES, SEQ], U8, align_bytes=64)
+            return codes, planes
+
+        def quantise(grouped, codes, planes, blocks, m=None):
+            flat_in = grouped[:].rearrange("p g m t -> p (g m t)")
+            flat_codes = codes[:].rearrange("p g m -> p (g m)")
+            flat_planes = planes[:].rearrange("p g m -> p (g m)")
+            if blocks == TILES:
+                nc.vector.quantize_mx(out=flat_codes.bitcast(FP8X4), scales=flat_planes, in_=flat_in)
+            else:
+                width = PASSES * P
+                nc.vector.quantize_mx(
+                    out=flat_codes[:, width * m : width * (m + 1)].bitcast(FP8X4),
+                    scales=flat_planes[:, width * m : width * (m + 1)],
+                    in_=flat_in[:, PACK * width * m : PACK * width * (m + 1)],
+                )
+
+        def new_queries():
+            qT = work.tile([P, CHUNKS, SEQ], F32)
+            return qT
+
+        def project_chunk(qT, codes, planes, blocks, c, engine="scalar"):
+            acc = psum.tile([P, SEQ], F32, tag="bank")
+            flat_codes = codes[:].rearrange("p g m -> p (g m)")
+            flat_planes = planes[:].rearrange("p g m -> p (g m)")
+            pieces = 1 if blocks == TILES else blocks
+            for m in range(pieces):
+                for g in range(PASSES):
+                    if blocks == TILES:
+                        columns = slice(SEQ * g, SEQ * (g + 1))
+                        target = acc[:]
+                    else:
+                        columns = slice(P * (PASSES * m + g), P * (PASSES * m + g + 1))
+                        target = acc[:, P * m : P * (m + 1)]
+                    nc.tensor.matmul_mx(
+                        out=target,
+                        lhsT=w_words[:, g, 2 * P * c : 2 * P * (c + 1)].bitcast(FP4X4),
+                        lhsT_scale=w_planes[:, g, P * c : P * (c + 1)],
+                        rhs=flat_codes[:, columns].bitcast(FP8X4),
+                        rhs_scale=flat_planes[:, columns],
+                        start=(g == 0),
+                        stop=(g == PASSES - 1),
+                    )
+            if engine == "scalar":
+                nc.scalar.activation(
+                    out=qT[:, c, 0 : P * blocks],
+                    in_=acc[:, 0 : P * blocks],
+                    func=ACT.Identity,
+                    bias=bias_col[:, c : c + 1],
+                    scale=SCORE_SCALE,
+                )
+            else:
+                nc.vector.tensor_scalar(
+                    out=qT[:, c, 0 : P * blocks],
+                    in0=acc[:, 0 : P * blocks],
+                    scalar1=SCORE_SCALE,
+                    scalar2=bias_col[:, c : c + 1],
+                    op0=ALU.mult,
+                    op1=ALU.add,
+                )
+
+        def new_keys(first, blocks):
+            kT = work.tile([P, CHUNKS, PAD + SEQ + PAD], F32)
+            if first % TILES == 0:
+                nc.gpsimd.memset(kT[:, :, 0:PAD], 0.0)
+            nc.gpsimd.memset(kT[:, :, PAD + P * blocks : PAD + P * blocks + PAD], 0.0)
+            return kT
+
+        def transpose_keys(kT, first, m, engine="scalar"):
+            kT_ps = psum.tile([P, CHUNKS, P], BF16, tag="bank")
+            for c in range(CHUNKS):
+                nc.tensor.transpose(kT_ps[:, c, :], k_sb[:, first + m - RUN + 1, P * c : P * (c + 1)], ident_bf[:])
+            if m < 0:
+                copy_out(engine, kT[:, :, PAD - NB : PAD], kT_ps[:, :, P - NB : P])
+            else:
+                copy_out(engine, kT[:, :, PAD + P * m : PAD + P * (m + 1)], kT_ps[:])
+
+        def band_block(qT, kT, first, m):
+            block = psum.tile([P, WINDOW], F32, tag="bank")
+            first_key = PAD - NB + P * m
+            for c in range(CHUNKS):
+                nc.tensor.matmul(
+                    out=block[:],
+                    lhsT=qT[:, c, P * m : P * (m + 1)],
+                    rhs=kT[:, c, first_key : first_key + WINDOW],
+                    start=(c == 0),
+                    stop=(c == CHUNKS - 1),
+                )
+            return block
+
+        def band_mask(block, first, m):
+            t = first + m
+            nc.vector.tensor_mul(out=banded[:, t // TILES % 2, t % TILES, 0:WINDOW], in0=block[:], in1=in_band[:])
+
+        def band_chain(first, blocks):
+            lo = first % TILES
+            folded = work.tile([P, TILES, BAND], F32)
+            low = work.tile([P, TILES], F32)
+            turned = work.tile([P, TILES, REPEATS, BAND], F32)
+            total = work.tile([P, TILES], F32)
+            share = work.tile([P, TILES, BAND], F32)
+            windows = work.tile([P, TILES, BAND, BAND], F32)
+            weights = work.tile([P, TILES, BAND], F32)
+            paired = work.tile([P, TILES, PAIR, BAND], F32)
+
+            def fold():
+                nc.vector.tensor_reduce(
+                    out=folded[:, 0:blocks, :],
+                    in_=banded[:, first // TILES % 2, lo : lo + blocks, :].rearrange("p n (a r) -> p n r a", r=BAND),
+                    axis=AXIS.X,
+                    op=ALU.add,
+                )
+                nc.vector.tensor_reduce(out=low[:, 0:blocks], in_=folded[:, 0:blocks, :], axis=AXIS.X, op=ALU.min)
+
+            def exps():
+                for n in range(blocks):
+                    nc.scalar.activation(
+                        out=turned[:, n, :, :],
+                        in_=folded[:, n, :].unsqueeze(1).to_broadcast([P, REPEATS, BAND]),
+                        func=ACT.Exp,
+                        scale=-1.0,
+                        bias=low[:, n : n + 1],
+                        accum_out=total[:, n : n + 1],
+                    )
+
+            def turn_back():
+                nc.vector.reciprocal(out=total[:, 0:blocks], in_=total[:, 0:blocks])
+                nc.vector.tensor_mul(
+                    out=share[:, 0:blocks, :],
+                    in0=turn[:].unsqueeze(1).to_broadcast([P, blocks, BAND]),
+                    in1=total[:, 0:blocks].unsqueeze(2).to_broadcast([P, blocks, BAND]),
+                )
+                nc.vector.tensor_mul(
+                    out=windows[:, 0:blocks],
+                    in0=turned[:, 0:blocks]
+                    .rearrange("p n a r -> p n (a r)")
+                    .rearrange("p n (s c) -> p n s c", c=REPEATS)[:, :, :, 0:BAND],
+                    in1=share[:, 0:blocks, :].unsqueeze(3).to_broadcast([P, blocks, BAND, BAND]),
+                )
+                nc.vector.tensor_reduce(
+                    out=weights[:, 0:blocks, :],
+                    in_=windows[:, 0:blocks].rearrange("p n s j -> p n j s"),
+                    axis=AXIS.X,
+                    op=ALU.add,
+                )
+
+            def store():
+                paired_ps = psum.tile([P, PAIR, TILES * BAND], F32, tag="bank")
+                for e in range(PAIR):
+                    nc.tensor.matmul(
+                        out=paired_ps[:, e, 0 : blocks * BAND],
+                        lhsT=pick[:, e, :],
+                        rhs=weights[:, 0:blocks, :].rearrange("p n j -> p (n j)"),
+                        start=True,
+                        stop=True,
+                    )
+                nc.vector.tensor_copy(
+                    out=paired[:, 0:blocks],
+                    in_=paired_ps[:, :, 0 : blocks * BAND].rearrange("p e (n j) -> p n e j", j=BAND),
+                )
+                nc.sync.dma_start(
+                    out=out_rows[P * first : P * (first + blocks)].rearrange(
+                        "(n m e) j -> m n (e j)", m=P // PAIR, e=PAIR
+                    ),
+                    in_=paired[0 : P // PAIR, 0:blocks].rearrange("m n e j -> m n (e j)"),
+                )
+
+            return [fold, exps, turn_back, store]
+
+        units = [(i, j) for i in range(RUN) for j in range(BAND)]
+        links = []
+        run_links = []
+
+        def products(done, count):
+            for i, j in units[done : done + count]:
+                run_product(i, j)
+            if done < len(units) <= done + count:
+                run_links.extend(run_chain())
+            return done + count
+
+        def share_of(total, parts, index):
+            return range(total * index // parts, total * (index + 1) // parts)
+
+        def prepare_x(first, blocks):
+            grouped = new_x()
+            codes, planes = new_codes()
+            for m in range(blocks):
+                transpose_x(grouped, first, blocks, m)
+                if blocks < TILES:
+                    quantise(grouped, codes, planes, blocks, m)
+            if blocks == TILES:
+                quantise(grouped, codes, planes, blocks)
+            return codes, planes
+
+        def project(qT, codes, planes, blocks):
+            for c in range(CHUNKS):
+                project_chunk(qT, codes, planes, blocks, c, "scalar" if c % 2 == 0 else EVEN_ENGINE)
+
+        setup_gpsimd()
+        bias_column()
+        run_transpose(0)
+        run_quantise(0)
+        for h in range(HALVES):
+            bias_row(h)
+        for i in range(1, RUN):
+            run_transpose(i)
+            run_quantise(i)
+        for h in range(HALVES):
+            for i in range(RUN):
+                run_project(i, h)
+        setup_run_mask()
+        first, blocks = groups[0]
+        codes, planes = prepare_x(first, blocks)
+        setup_band()
+        kT = new_keys(first, blocks)
+        if halo_block:
+            transpose_keys(kT, first, -1)
+        for m in range(blocks):
+            transpose_keys(kT, first, m)
+        qT = new_queries()
+        project(qT, codes, planes, blocks)
+        done = products(0, PRODUCTS_HEAD)
+        served = 0
+        run_served = 0
+        for index, (first, blocks) in enumerate(groups):
+            following = groups[index + 1] if index + 1 < len(groups) else None
+            if following:
+                codes, planes = prepare_x(following[0], following[1])
+                next_kT = new_keys(following[0], following[1])
+                next_qT = new_queries()
+            for m in range(blocks):
+                if following and m == blocks - 1:
+                    project(next_qT, codes, planes, following[1])
+                block = band_block(qT, kT, first, m)
+                done = products(done, PRODUCTS_PER_BLOCK)
+                band_mask(block, first, m)
+                if served < len(links):
+                    links[served]()
+                    served += 1
+                if run_served < len(run_links):
+                    run_links[run_served]()
+                    run_served += 1
+                if following:
+                    for n in share_of(following[1], blocks, m):
+                        transpose_keys(next_kT, following[0], n)
+            if following:
                 kT = next_kT
-                qT = project_batch(codes, planes)
-            weights = softmax_rows(band_scores())
-        store_blocks(BATCHES - 1, weights)
+                qT = next_qT
+                links.extend(band_chain(first, blocks))
+            else:
+                links.extend(band_chain(first, blocks))
+        done = products(done, len(units))
+        for link in run_links[run_served:] + links[served:]:
+            link()

@@ -229,9 +229,9 @@ def tile_crosssliceattention_pa_kernel(tc, x, Wq_words, Wq_scales, bq, k_proj, o
                         nc.tensor.transpose(xT[:, g, u, :], sort[:, g, u, :], ident[:])
             return xT
 
-        def sort_words(tokens, engine):
-            x_sorted = work.tile([P, PASSES, 2, P], F32, bufs=SORT_BUFS)
-            copy_out(engine, x_sorted[:], tokens.bitcast(F32).rearrange("t (g p u) -> t g u p", g=PASSES, u=2))
+        def sort_words(tokens, engine, place):
+            x_sorted = x_run[:, place, :].bitcast(F32).rearrange("t (g u p) -> t g u p", g=PASSES, u=2)
+            copy_out(engine, x_sorted, tokens.bitcast(F32).rearrange("t (g p u) -> t g u p", g=PASSES, u=2))
             return x_sorted
 
         q_run = keep.tile([P, RUN, D], F32)
@@ -514,11 +514,14 @@ def tile_crosssliceattention_pa_kernel(tc, x, Wq_words, Wq_scales, bq, k_proj, o
         def share_of(total, parts, index):
             return range(total * index // parts, total * (index + 1) // parts)
 
-        def prepare_x(first, blocks):
+        def sort_x(group, m, engine):
+            return sort_words(x_sb[:, group[0] + m - RUN, :], engine, (group[0] + m) % RUN) if engine else None
+
+        def prepare_x(first, blocks, sorts):
             grouped = new_x()
             codes, planes = new_codes()
             for m in range(blocks):
-                transpose_x(grouped, first, blocks, m)
+                transpose_x(grouped, first, blocks, m, "scalar", sorts[m])
                 if blocks < TILES:
                     quantise(grouped, codes, planes, blocks, m)
             if blocks == TILES:
@@ -543,7 +546,7 @@ def tile_crosssliceattention_pa_kernel(tc, x, Wq_words, Wq_scales, bq, k_proj, o
                 run_project(i, h)
         setup_run_mask()
         first, blocks = groups[0]
-        codes, planes = prepare_x(first, blocks)
+        codes, planes = prepare_x(first, blocks, [sort_x(groups[0], m, None) for m in range(blocks)])
         setup_band()
         kT = new_keys(first, blocks)
         if halo_block:
@@ -552,13 +555,16 @@ def tile_crosssliceattention_pa_kernel(tc, x, Wq_words, Wq_scales, bq, k_proj, o
             transpose_keys(kT, first, m)
         qT = new_queries()
         project(qT, codes, planes, blocks)
+        sorts = [sort_x(groups[1], m, None) for m in range(groups[1][1])]
         done = products(0, PRODUCTS_HEAD)
         served = 0
         run_served = 0
         for index, (first, blocks) in enumerate(groups):
             following = groups[index + 1] if index + 1 < len(groups) else None
+            later = groups[index + 2] if index + 2 < len(groups) else None
             if following:
-                codes, planes = prepare_x(following[0], following[1])
+                codes, planes = prepare_x(following[0], following[1], sorts)
+                sorts = []
                 next_kT = new_keys(following[0], following[1])
                 next_qT = new_queries()
             for m in range(blocks):
@@ -576,6 +582,8 @@ def tile_crosssliceattention_pa_kernel(tc, x, Wq_words, Wq_scales, bq, k_proj, o
                 if following:
                     for n in share_of(following[1], blocks, m):
                         transpose_keys(next_kT, following[0], n)
+                if later:
+                    sorts.extend([sort_x(later, n, "scalar") for n in share_of(later[1], blocks, m)])
             if following:
                 kT = next_kT
                 qT = next_qT

@@ -456,6 +456,20 @@ def tile_crosssliceattention_pa_kernel(tc, x, Wq_words, Wq_scales, bq, k_proj, o
                         accum_out=total[:, n : n + 1],
                     )
 
+            def turn_back_one():
+                nc.vector.reciprocal(out=total[:, 0:1], in_=total[:, 0:1])
+                nc.vector.scalar_tensor_tensor(
+                    out=windows[:, 0],
+                    in0=turned[:, 0].rearrange("p a r -> p (a r)").rearrange("p (s c) -> p s c", c=REPEATS)[:, :, 0:BAND],
+                    scalar=total[:, 0:1],
+                    in1=turn[:].unsqueeze(2).to_broadcast([P, BAND, BAND]),
+                    op0=ALU.mult,
+                    op1=ALU.mult,
+                )
+                nc.vector.tensor_reduce(
+                    out=weights[:, 0, :], in_=windows[:, 0].rearrange("p s j -> p j s"), axis=AXIS.X, op=ALU.add
+                )
+
             def turn_back():
                 nc.vector.reciprocal(out=total[:, 0:blocks], in_=total[:, 0:blocks])
                 nc.vector.tensor_mul(
@@ -498,7 +512,7 @@ def tile_crosssliceattention_pa_kernel(tc, x, Wq_words, Wq_scales, bq, k_proj, o
                     in_=paired[0 : P // PAIR, 0:blocks].rearrange("m n e j -> m n (e j)"),
                 )
 
-            return [fold, exps, turn_back, store]
+            return [fold, exps, turn_back_one if blocks == 1 else turn_back, store]
 
         units = [(i, j) for i in range(RUN) for j in range(BAND)]
         links = []
@@ -582,6 +596,10 @@ def tile_crosssliceattention_pa_kernel(tc, x, Wq_words, Wq_scales, bq, k_proj, o
                 if following:
                     for n in share_of(following[1], blocks, m):
                         transpose_keys(next_kT, following[0], n)
+                elif m == blocks - 2:
+                    early = band_chain(first, blocks - 1)
+                    early[0]()
+                    early[1]()
                 if later:
                     sorts.extend([sort_x(later, n, "scalar") for n in share_of(later[1], blocks, m)])
             if following:
@@ -589,7 +607,8 @@ def tile_crosssliceattention_pa_kernel(tc, x, Wq_words, Wq_scales, bq, k_proj, o
                 qT = next_qT
                 links.extend(band_chain(first, blocks))
             else:
-                links.extend(band_chain(first, blocks))
+                late = band_chain(first + blocks - 1, 1)
+                links.extend([late[0], late[1], early[2], late[2], early[3], late[3]])
         done = products(done, len(units))
         for link in run_links[run_served:] + links[served:]:
             link()

@@ -66,8 +66,11 @@ def tile_crosssliceattention_pa_kernel(tc, x, Wq_words, Wq_scales, bq, k_proj, o
         w_words = keep.tile([P, PASSES, 2 * D], U8, align_bytes=64)
         w_planes = keep.tile([P, PASSES, D], U8, align_bytes=64)
         bias_raw = keep.tile([CHUNKS, P], BF16)
+        bias_top = keep.tile([P, D], BF16)
+        ones = keep.tile([P, P], BF16)
 
         nc.vector.memset(w_planes[:].bitcast(I32), 0)
+        nc.gpsimd.memset(bias_top[:], 0.0)
 
         def load_x_run(i):
             nc.sync.dma_start(out=x_run[:, i, :], in_=x_rows[0 : P * RUN].rearrange("(p i) k -> p i k", i=RUN)[:, i, :])
@@ -111,6 +114,7 @@ def tile_crosssliceattention_pa_kernel(tc, x, Wq_words, Wq_scales, bq, k_proj, o
             after = k_rows[RUN : RUN + P * RUN].rearrange("(p i) d -> p i d", i=RUN)
             nc.sync.dma_start(out=k_run[:, SLOTS - NB : SLOTS, :], in_=after[:, 0:NB, :])
 
+        nc.sync.dma_start(out=bias_top[0:1, :], in_=bq.rearrange("(o n) -> o n", o=1))
         nc.sync.dma_start(out=bias_raw[:], in_=bq.rearrange("(c f) -> c f", f=P))
         load_x_run(0)
         load_x_run(1)
@@ -145,6 +149,7 @@ def tile_crosssliceattention_pa_kernel(tc, x, Wq_words, Wq_scales, bq, k_proj, o
 
         def setup_gpsimd():
             make_identity(nc, ident[:])
+            nc.gpsimd.memset(ones[:], 1.0)
             nc.gpsimd.memset(bias_rows[:], 0.0)
             nc.gpsimd.memset(warm[:], 0.0)
             nc.scalar.activation(out=warm[:], in_=warm[:], func=ACT.Exp)
@@ -204,12 +209,10 @@ def tile_crosssliceattention_pa_kernel(tc, x, Wq_words, Wq_scales, bq, k_proj, o
 
         def bias_row(h):
             wide_ps = psum.tile([P, BANK], F32, tag="bank")
-            for c in range(BANK // P):
-                chunk = (BANK // P) * h + c
-                nc.tensor.transpose(
-                    wide_ps[:, P * c : P * (c + 1)], bias_col[:, chunk : chunk + 1].to_broadcast([P, P]), ident[:]
-                )
-            nc.vector.tensor_copy(out=bias_wide[:, BANK * h : BANK * (h + 1)], in_=wide_ps[:])
+            nc.tensor.matmul(
+                out=wide_ps[:], lhsT=ones[:], rhs=bias_top[:, BANK * h : BANK * (h + 1)], start=True, stop=True
+            )
+            nc.scalar.mul(out=bias_wide[:, BANK * h : BANK * (h + 1)], in_=wide_ps[:], mul=SCORE_SCALE)
 
         def copy_out(engine, out_ap, in_ap):
             if engine == "scalar":
@@ -236,19 +239,20 @@ def tile_crosssliceattention_pa_kernel(tc, x, Wq_words, Wq_scales, bq, k_proj, o
 
         q_run = keep.tile([P, RUN, D], F32)
         run_scores = keep.tile([P, RUN, BAND], F32)
-        run_grouped = keep.tile([P, RUN, PASSES, P, PACK], BF16, align_bytes=64)
         run_codes = keep.tile([P, RUN, PASSES, P], U32, align_bytes=64)
         run_planes = keep.tile([P, RUN, PASSES, P], U8, align_bytes=64)
 
         def run_transpose(i, engine="scalar", sort=None):
             xT = transpose_words(x_run[:, i, :], sort)
-            copy_out(engine, run_grouped[:].bitcast(F32)[:, i], xT[:].rearrange("p g u m -> p g m u"))
+            run_grouped = work.tile([P, PASSES, P, PACK], BF16, align_bytes=64, bufs=3)
+            copy_out(engine, run_grouped[:].bitcast(F32), xT[:].rearrange("p g u m -> p g m u"))
+            return run_grouped
 
-        def run_quantise(i):
+        def run_quantise(i, run_grouped):
             nc.vector.quantize_mx(
                 out=run_codes[:, i].rearrange("p g m -> p (g m)").bitcast(FP8X4),
                 scales=run_planes[:, i].rearrange("p g m -> p (g m)"),
-                in_=run_grouped[:, i].rearrange("p g m t -> p (g m t)"),
+                in_=run_grouped[:].rearrange("p g m t -> p (g m t)"),
             )
 
         def run_project(i, h):
@@ -547,14 +551,12 @@ def tile_crosssliceattention_pa_kernel(tc, x, Wq_words, Wq_scales, bq, k_proj, o
                 project_chunk(qT, codes, planes, blocks, c, "scalar" if c % 2 == 0 else EVEN_ENGINE)
 
         setup_gpsimd()
-        bias_column()
-        run_transpose(0)
-        run_quantise(0)
+        run_quantise(0, run_transpose(0))
         for h in range(HALVES):
             bias_row(h)
         for i in range(1, RUN):
-            run_transpose(i)
-            run_quantise(i)
+            run_quantise(i, run_transpose(i))
+        bias_column()
         for h in range(HALVES):
             for i in range(RUN):
                 run_project(i, h)

@@ -278,7 +278,7 @@ def tile_crosssliceattention_pa_kernel(tc, x, Wq_words, Wq_scales, bq, k_proj, o
             )
 
         def run_product(i, j):
-            products = work.tile([P, D], F32, bufs=2)
+            products = work.tile([P, D], F32, bufs=3)
             nc.vector.scalar_tensor_tensor(
                 out=products[:],
                 in0=q_run[:, i, :],
@@ -505,11 +505,11 @@ def tile_crosssliceattention_pa_kernel(tc, x, Wq_words, Wq_scales, bq, k_proj, o
                         start=True,
                         stop=True,
                     )
-                nc.vector.tensor_copy(
+                nc.scalar.copy(
                     out=paired[:, 0:blocks],
                     in_=paired_ps[:, :, 0 : blocks * BAND].rearrange("p e (n j) -> p n e j", j=BAND),
                 )
-                nc.sync.dma_start(
+                nc.scalar.dma_start(
                     out=out_rows[P * first : P * (first + blocks)].rearrange(
                         "(n m e) j -> m n (e j)", m=P // PAIR, e=PAIR
                     ),

@@ -31,9 +31,12 @@ PSUM_BANKS = 8
 HALVES = D // BANK
 PAD = 8
 WINDOW = P + 2 * NB
-FOLDS = -(-WINDOW // BAND)
-REPEATS = BAND + 1
-PAIR = 2
+RESIDUES = BAND + 1
+FOLDS = WINDOW // RESIDUES
+RUN_COLUMNS = FOLDS + 2
+REPEATS = RESIDUES + 1
+GATHER = 8
+RUN_GATHER = 4
 SCORE_SCALE = 1.0 / math.sqrt(D)
 MASKED = -1.0e30
 HALO_CUT = 112
@@ -138,11 +141,15 @@ def tile_crosssliceattention_pa_kernel(tc, x, Wq_words, Wq_scales, bq, k_proj, o
         ident = keep.tile([P, P], F32)
         ident_bf = keep.tile([P, P], BF16)
         warm = keep.tile([P, 1], F32)
-        pick = keep.tile([P, PAIR, P], F32)
+        pick = keep.tile([P, P], F32)
+        place = keep.tile([P, GATHER], F32)
+        run_pick = keep.tile([P, P], F32)
+        run_place = keep.tile([P, RUN_GATHER], F32)
         run_mask = keep.tile([P, RUN, BAND], F32)
-        in_band = keep.tile([P, WINDOW], F32)
-        banded = keep.tile([P, 2, TILES, (FOLDS + 1) * BAND], F32)
-        turn = keep.tile([P, BAND], F32)
+        band = keep.tile([P, WINDOW], F32)
+        in_band = keep.tile([P, RESIDUES, FOLDS], F32)
+        banded = keep.tile([P, 2, TILES, RESIDUES, RUN_COLUMNS], F32)
+        turn = keep.tile([P, RESIDUES], F32)
         bias_rows = keep.tile([P, P], F32)
         bias_col = keep.tile([P, CHUNKS], F32)
         bias_wide = keep.tile([P, D], F32)
@@ -157,30 +164,51 @@ def tile_crosssliceattention_pa_kernel(tc, x, Wq_words, Wq_scales, bq, k_proj, o
             make_identity(nc, ident_bf[:])
             nc.gpsimd.memset(run_mask[:], 0.0)
             nc.gpsimd.memset(in_band[:], 0.0)
+            nc.gpsimd.memset(band[:], 0.0)
             nc.gpsimd.memset(banded[:], 0.0)
             nc.gpsimd.memset(pick[:], 0.0)
             for j in range(BAND):
-                nc.gpsimd.tensor_tensor(
-                    out=in_band[:, j : j + P], in0=in_band[:, j : j + P], in1=ident[:], op=ALU.subtract
-                )
-            nc.gpsimd.tensor_copy(out=pick[:, :, 0 : P // PAIR], in_=ident[:].rearrange("p (m e) -> p e m", e=PAIR))
+                nc.gpsimd.tensor_tensor(out=band[:, j : j + P], in0=band[:, j : j + P], in1=ident[:], op=ALU.subtract)
+            nc.gpsimd.memset(run_pick[:], 0.0)
             nc.gpsimd.tensor_scalar(
-                out=banded[:, 0, 0, 0:P], in0=ident[:], scalar1=float(REPEATS), scalar2=0.0, op0=ALU.mult, op1=ALU.add
+                out=in_band[:].rearrange("p r a -> p (r a)")[:, 0:P],
+                in0=ident[:],
+                scalar1=float(REPEATS),
+                scalar2=0.0,
+                op0=ALU.mult,
+                op1=ALU.add,
             )
 
         def setup_band():
             nc.vector.tensor_reduce(
-                out=turn[:], in_=banded[:, 0, 0, :].rearrange("p (a r) -> p r a", r=BAND), axis=AXIS.X, op=ALU.add
+                out=turn[:],
+                in_=in_band[:].rearrange("p r a -> p (r a)").rearrange("p (a r) -> p r a", r=RESIDUES),
+                axis=AXIS.X,
+                op=ALU.add,
             )
+            nc.vector.tensor_copy(out=in_band[:], in_=band[:].rearrange("p (a r) -> p r a", r=RESIDUES))
+            both = banded[:].rearrange("p c n r a -> p (c n) r a")
+            for low, high, start in ((0, RESIDUES - 1, 1), (RESIDUES - 1, RESIDUES, 0)):
+                shape = [P, 2 * TILES, high - low]
+                nc.vector.tensor_scalar_mul(
+                    out=both[:, :, low:high, FOLDS],
+                    in0=turn[:, start : start + high - low].unsqueeze(1).to_broadcast(shape),
+                    scalar1=-MASKED,
+                )
+            for picks, places, count in ((pick, place, GATHER), (run_pick, run_place, RUN_GATHER)):
+                by_row = ident[:].rearrange("p (r e) -> p r e", e=count)
+                nc.vector.tensor_reduce(out=picks[:, 0 : P // count], in_=by_row, axis=AXIS.X, op=ALU.add)
+                by_place = ident[:].rearrange("p (r e) -> p e r", e=count)
+                nc.vector.tensor_reduce(out=places[:], in_=by_place, axis=AXIS.X, op=ALU.add)
             for i in range(NB):
                 for t in range(NB - i):
                     for n, m, w in ((0, i, i + t), (TILES - 1, P - 1 - i, P - 1 - i + BAND - 1 - t)):
-                        place = FOLDS * BAND + w % BAND
+                        spot = (w % RESIDUES, FOLDS)
                         nc.vector.scalar_tensor_tensor(
-                            out=banded[:, :, n, place],
+                            out=banded[:, :, n, spot[0], spot[1]],
                             in0=ident[:, m : m + 1].to_broadcast([P, 2]),
                             scalar=-MASKED,
-                            in1=banded[:, :, n, place],
+                            in1=banded[:, :, n, spot[0], spot[1]],
                             op0=ALU.mult,
                             op1=ALU.add,
                         )
@@ -278,7 +306,7 @@ def tile_crosssliceattention_pa_kernel(tc, x, Wq_words, Wq_scales, bq, k_proj, o
             )
 
         def run_product(i, j):
-            products = work.tile([P, D], F32, bufs=3)
+            products = work.tile([P, D], F32, bufs=2)
             nc.vector.scalar_tensor_tensor(
                 out=products[:],
                 in0=q_run[:, i, :],
@@ -294,6 +322,8 @@ def tile_crosssliceattention_pa_kernel(tc, x, Wq_words, Wq_scales, bq, k_proj, o
             top = work.tile(rows, F32)
             run_weights = work.tile(rows + [BAND], F32)
             run_total = work.tile(rows, F32)
+            run_spread = work.tile([P, RUN_GATHER, RUN * BAND], F32)
+            run_gathered = work.tile([P, RUN_GATHER * RUN * BAND], F32)
 
             def shift():
                 nc.vector.tensor_add(out=run_scores[:], in0=run_scores[:], in1=run_mask[:])
@@ -311,12 +341,30 @@ def tile_crosssliceattention_pa_kernel(tc, x, Wq_words, Wq_scales, bq, k_proj, o
                 nc.vector.tensor_mul(
                     out=run_weights[:], in0=run_weights[:], in1=run_total[:].unsqueeze(2).to_broadcast(rows + [BAND])
                 )
-                nc.sync.dma_start(
-                    out=out_rows[0 : P * RUN].rearrange("(p i) j -> p (i j)", i=RUN),
-                    in_=run_weights[:].rearrange("p i j -> p (i j)"),
+                shape = [P, RUN_GATHER, RUN * BAND]
+                nc.vector.tensor_mul(
+                    out=run_spread[:],
+                    in0=run_weights[:].rearrange("p i j -> p (i j)").unsqueeze(1).to_broadcast(shape),
+                    in1=run_place[:].unsqueeze(2).to_broadcast(shape),
                 )
 
-            return [shift, exps, divide]
+            def store():
+                run_ps = psum.tile([P, RUN_GATHER * RUN * BAND], F32, tag="bank")
+                nc.tensor.matmul(
+                    out=run_ps[:],
+                    lhsT=run_pick[:],
+                    rhs=run_spread[:].rearrange("p e c -> p (e c)"),
+                    start=True,
+                    stop=True,
+                )
+                runs = P // RUN_GATHER
+                nc.scalar.copy(out=run_gathered[0:runs, :], in_=run_ps[0:runs, :])
+                nc.scalar.dma_start(
+                    out=out_rows[0 : P * RUN].rearrange("(m e i) j -> m (e i j)", e=RUN_GATHER, i=RUN),
+                    in_=run_gathered[0:runs, :],
+                )
+
+            return [shift, exps, divide, store]
 
         def new_x():
             grouped = work.tile([P, PASSES, SEQ, PACK], BF16, align_bytes=64)
@@ -396,12 +444,16 @@ def tile_crosssliceattention_pa_kernel(tc, x, Wq_words, Wq_scales, bq, k_proj, o
                     op1=ALU.add,
                 )
 
-        def new_keys(first, blocks):
-            kT = work.tile([P, CHUNKS, PAD + SEQ + PAD], F32)
-            if first % TILES == 0:
+        kT_even = keep.tile([P, CHUNKS, PAD + SEQ + PAD], F32)
+        kT_odd = keep.tile([P, CHUNKS, PAD + SEQ + PAD], F32)
+
+        def setup_pads():
+            for kT in (kT_even, kT_odd):
                 nc.gpsimd.memset(kT[:, :, 0:PAD], 0.0)
-            nc.gpsimd.memset(kT[:, :, PAD + P * blocks : PAD + P * blocks + PAD], 0.0)
-            return kT
+                nc.gpsimd.memset(kT[:, :, PAD + SEQ : PAD + SEQ + PAD], 0.0)
+            short = PAD + P * groups[0][1]
+            if short < PAD + SEQ:
+                nc.gpsimd.memset(kT_even[:, :, short : short + PAD], 0.0)
 
         def transpose_keys(kT, first, m, engine="scalar"):
             kT_ps = psum.tile([P, CHUNKS, P], BF16, tag="bank")
@@ -427,67 +479,64 @@ def tile_crosssliceattention_pa_kernel(tc, x, Wq_words, Wq_scales, bq, k_proj, o
 
         def band_mask(block, first, m):
             t = first + m
-            nc.vector.tensor_mul(out=banded[:, t // TILES % 2, t % TILES, 0:WINDOW], in0=block[:], in1=in_band[:])
+            nc.vector.tensor_mul(
+                out=banded[:, t // TILES % 2, t % TILES, :, 0:FOLDS],
+                in0=block[:].rearrange("p (a r) -> p r a", r=RESIDUES),
+                in1=in_band[:],
+            )
 
         def band_chain(first, blocks):
             lo = first % TILES
-            folded = work.tile([P, TILES, BAND], F32)
+            folded = work.tile([P, TILES, RESIDUES], F32)
             low = work.tile([P, TILES], F32)
-            turned = work.tile([P, TILES, REPEATS, BAND], F32)
+            turned = work.tile([P, TILES, REPEATS, RESIDUES], F32)
             total = work.tile([P, TILES], F32)
-            share = work.tile([P, TILES, BAND], F32)
-            windows = work.tile([P, TILES, BAND, BAND], F32)
+            share = work.tile([P, TILES, GATHER], F32)
+            windows = work.tile([P, TILES, RESIDUES, BAND], F32)
             weights = work.tile([P, TILES, BAND], F32)
-            paired = work.tile([P, TILES, PAIR, BAND], F32)
+            spread = work.tile([P, TILES, GATHER, BAND], F32)
+            gathered = work.tile([P, TILES, GATHER, BAND], F32)
 
             def fold():
                 nc.vector.tensor_reduce(
                     out=folded[:, 0:blocks, :],
-                    in_=banded[:, first // TILES % 2, lo : lo + blocks, :].rearrange("p n (a r) -> p n r a", r=BAND),
+                    in_=banded[:, first // TILES % 2, lo : lo + blocks, :, 0 : FOLDS + 1],
                     axis=AXIS.X,
                     op=ALU.add,
                 )
+
+            def lowest():
                 nc.vector.tensor_reduce(out=low[:, 0:blocks], in_=folded[:, 0:blocks, :], axis=AXIS.X, op=ALU.min)
 
             def exps():
                 for n in range(blocks):
                     nc.scalar.activation(
                         out=turned[:, n, :, :],
-                        in_=folded[:, n, :].unsqueeze(1).to_broadcast([P, REPEATS, BAND]),
+                        in_=folded[:, n, :].unsqueeze(1).to_broadcast([P, REPEATS, RESIDUES]),
                         func=ACT.Exp,
                         scale=-1.0,
                         bias=low[:, n : n + 1],
                         accum_out=total[:, n : n + 1],
                     )
 
-            def turn_back_one():
-                nc.vector.reciprocal(out=total[:, 0:1], in_=total[:, 0:1])
-                nc.vector.scalar_tensor_tensor(
-                    out=windows[:, 0],
-                    in0=turned[:, 0].rearrange("p a r -> p (a r)").rearrange("p (s c) -> p s c", c=REPEATS)[:, :, 0:BAND],
-                    scalar=total[:, 0:1],
-                    in1=turn[:].unsqueeze(2).to_broadcast([P, BAND, BAND]),
-                    op0=ALU.mult,
-                    op1=ALU.mult,
-                )
-                nc.vector.tensor_reduce(
-                    out=weights[:, 0, :], in_=windows[:, 0].rearrange("p s j -> p j s"), axis=AXIS.X, op=ALU.add
-                )
-
-            def turn_back():
+            def invert():
                 nc.vector.reciprocal(out=total[:, 0:blocks], in_=total[:, 0:blocks])
                 nc.vector.tensor_mul(
                     out=share[:, 0:blocks, :],
-                    in0=turn[:].unsqueeze(1).to_broadcast([P, blocks, BAND]),
-                    in1=total[:, 0:blocks].unsqueeze(2).to_broadcast([P, blocks, BAND]),
+                    in0=place[:].unsqueeze(1).to_broadcast([P, blocks, GATHER]),
+                    in1=total[:, 0:blocks].unsqueeze(2).to_broadcast([P, blocks, GATHER]),
                 )
+
+            def turn_back():
                 nc.vector.tensor_mul(
                     out=windows[:, 0:blocks],
                     in0=turned[:, 0:blocks]
                     .rearrange("p n a r -> p n (a r)")
                     .rearrange("p n (s c) -> p n s c", c=REPEATS)[:, :, :, 0:BAND],
-                    in1=share[:, 0:blocks, :].unsqueeze(3).to_broadcast([P, blocks, BAND, BAND]),
+                    in1=turn[:].unsqueeze(1).unsqueeze(3).to_broadcast([P, blocks, RESIDUES, BAND]),
                 )
+
+            def weigh():
                 nc.vector.tensor_reduce(
                     out=weights[:, 0:blocks, :],
                     in_=windows[:, 0:blocks].rearrange("p n s j -> p n j s"),
@@ -495,28 +544,33 @@ def tile_crosssliceattention_pa_kernel(tc, x, Wq_words, Wq_scales, bq, k_proj, o
                     op=ALU.add,
                 )
 
-            def store():
-                paired_ps = psum.tile([P, PAIR, TILES * BAND], F32, tag="bank")
-                for e in range(PAIR):
-                    nc.tensor.matmul(
-                        out=paired_ps[:, e, 0 : blocks * BAND],
-                        lhsT=pick[:, e, :],
-                        rhs=weights[:, 0:blocks, :].rearrange("p n j -> p (n j)"),
-                        start=True,
-                        stop=True,
-                    )
-                nc.scalar.copy(
-                    out=paired[:, 0:blocks],
-                    in_=paired_ps[:, :, 0 : blocks * BAND].rearrange("p e (n j) -> p n e j", j=BAND),
-                )
-                nc.scalar.dma_start(
-                    out=out_rows[P * first : P * (first + blocks)].rearrange(
-                        "(n m e) j -> m n (e j)", m=P // PAIR, e=PAIR
-                    ),
-                    in_=paired[0 : P // PAIR, 0:blocks].rearrange("m n e j -> m n (e j)"),
+            def spread_out():
+                nc.vector.tensor_mul(
+                    out=spread[:, 0:blocks],
+                    in0=weights[:, 0:blocks, :].unsqueeze(2).to_broadcast([P, blocks, GATHER, BAND]),
+                    in1=share[:, 0:blocks, :].unsqueeze(3).to_broadcast([P, blocks, GATHER, BAND]),
                 )
 
-            return [fold, exps, turn_back_one if blocks == 1 else turn_back, store]
+            def store():
+                gathered_ps = psum.tile([P, TILES, GATHER * BAND], F32, tag="bank")
+                nc.tensor.matmul(
+                    out=gathered_ps[:, 0:blocks].rearrange("p n c -> p (n c)"),
+                    lhsT=pick[:],
+                    rhs=spread[:, 0:blocks].rearrange("p n e j -> p (n e j)"),
+                    start=True,
+                    stop=True,
+                )
+                rows = P // GATHER
+                nc.scalar.copy(
+                    out=gathered[0:rows, 0:blocks].rearrange("p n e j -> p (n e j)"),
+                    in_=gathered_ps[0:rows, 0:blocks].rearrange("p n c -> p (n c)"),
+                )
+                nc.scalar.dma_start(
+                    out=out_rows[P * first : P * (first + blocks)].rearrange("(n m e) j -> m n (e j)", m=rows, e=GATHER),
+                    in_=gathered[0:rows, 0:blocks].rearrange("m n e j -> m n (e j)"),
+                )
+
+            return [lambda: (fold(), lowest()), exps, lambda: (turn_back(), invert(), weigh(), spread_out()), store]
 
         units = [(i, j) for i in range(RUN) for j in range(BAND)]
         links = []
@@ -551,6 +605,7 @@ def tile_crosssliceattention_pa_kernel(tc, x, Wq_words, Wq_scales, bq, k_proj, o
                 project_chunk(qT, codes, planes, blocks, c, "scalar" if c % 2 == 0 else EVEN_ENGINE)
 
         setup_gpsimd()
+        setup_pads()
         run_quantise(0, run_transpose(0))
         for h in range(HALVES):
             bias_row(h)
@@ -564,7 +619,7 @@ def tile_crosssliceattention_pa_kernel(tc, x, Wq_words, Wq_scales, bq, k_proj, o
         first, blocks = groups[0]
         codes, planes = prepare_x(first, blocks, [sort_x(groups[0], m, None) for m in range(blocks)])
         setup_band()
-        kT = new_keys(first, blocks)
+        kT = kT_even
         if halo_block:
             transpose_keys(kT, first, -1)
         for m in range(blocks):
@@ -581,7 +636,7 @@ def tile_crosssliceattention_pa_kernel(tc, x, Wq_words, Wq_scales, bq, k_proj, o
             if following:
                 codes, planes = prepare_x(following[0], following[1], sorts)
                 sorts = []
-                next_kT = new_keys(following[0], following[1])
+                next_kT = (kT_even, kT_odd)[(index + 1) % 2]
                 next_qT = new_queries()
             for m in range(blocks):
                 if following and m == blocks - 1:

@@ -73,7 +73,7 @@ def tile_crosssliceattention_pa_kernel(tc, x, Wq_words, Wq_scales, bq, k_proj, o
         ones = keep.tile([P, P], BF16)
 
         nc.vector.memset(w_planes[:].bitcast(I32), 0)
-        nc.gpsimd.memset(bias_top[:], 0.0)
+        nc.vector.memset(bias_top[:], 0.0)
 
         def load_x_run(i):
             nc.sync.dma_start(out=x_run[:, i, :], in_=x_rows[0 : P * RUN].rearrange("(p i) k -> p i k", i=RUN)[:, i, :])
@@ -117,15 +117,15 @@ def tile_crosssliceattention_pa_kernel(tc, x, Wq_words, Wq_scales, bq, k_proj, o
             after = k_rows[RUN : RUN + P * RUN].rearrange("(p i) d -> p i d", i=RUN)
             nc.sync.dma_start(out=k_run[:, SLOTS - NB : SLOTS, :], in_=after[:, 0:NB, :])
 
-        nc.sync.dma_start(out=bias_top[0:1, :], in_=bq.rearrange("(o n) -> o n", o=1))
-        nc.sync.dma_start(out=bias_raw[:], in_=bq.rearrange("(c f) -> c f", f=P))
         load_x_run(0)
+        nc.sync.dma_start(out=bias_raw[:], in_=bq.rearrange("(c f) -> c f", f=P))
+        nc.sync.dma_start(out=bias_top[0:1, :], in_=bq.rearrange("(o n) -> o n", o=1))
         load_x_run(1)
         load_scales()
         load_w(0)
+        load_w(1)
         for i in range(2, RUN):
             load_x_run(i)
-        load_w(1)
         for index, (first, blocks) in enumerate(groups):
             for m in range(blocks):
                 load_x(first + m)
@@ -146,9 +146,9 @@ def tile_crosssliceattention_pa_kernel(tc, x, Wq_words, Wq_scales, bq, k_proj, o
         run_pick = keep.tile([P, P], F32)
         run_place = keep.tile([P, RUN_GATHER], F32)
         run_mask = keep.tile([P, RUN, BAND], F32)
-        band = keep.tile([P, WINDOW], F32)
         in_band = keep.tile([P, RESIDUES, FOLDS], F32)
         banded = keep.tile([P, 2, TILES, RESIDUES, RUN_COLUMNS], F32)
+        starts = keep.tile([P, RESIDUES, FOLDS], F32)
         turn = keep.tile([P, RESIDUES], F32)
         bias_rows = keep.tile([P, P], F32)
         bias_col = keep.tile([P, CHUNKS], F32)
@@ -156,37 +156,39 @@ def tile_crosssliceattention_pa_kernel(tc, x, Wq_words, Wq_scales, bq, k_proj, o
 
         def setup_gpsimd():
             make_identity(nc, ident[:])
-            nc.gpsimd.memset(ones[:], 1.0)
-            nc.gpsimd.memset(bias_rows[:], 0.0)
             nc.gpsimd.memset(warm[:], 0.0)
             nc.scalar.activation(out=warm[:], in_=warm[:], func=ACT.Exp)
-            nc.gpsimd.memset(k_run[0:1, 0:NB, :], 0.0)
-            make_identity(nc, ident_bf[:])
-            nc.gpsimd.memset(run_mask[:], 0.0)
-            nc.gpsimd.memset(in_band[:], 0.0)
-            nc.gpsimd.memset(band[:], 0.0)
-            nc.gpsimd.memset(banded[:], 0.0)
-            nc.gpsimd.memset(pick[:], 0.0)
-            for j in range(BAND):
-                nc.gpsimd.tensor_tensor(out=band[:, j : j + P], in0=band[:, j : j + P], in1=ident[:], op=ALU.subtract)
-            nc.gpsimd.memset(run_pick[:], 0.0)
-            nc.gpsimd.tensor_scalar(
-                out=in_band[:].rearrange("p r a -> p (r a)")[:, 0:P],
-                in0=ident[:],
-                scalar1=float(REPEATS),
-                scalar2=0.0,
-                op0=ALU.mult,
-                op1=ALU.add,
+            nc.gpsimd.memset(ones[:], 1.0)
+            nc.gpsimd.memset(bias_rows[:], 0.0)
+            key = [[1, RESIDUES], [RESIDUES, FOLDS]]
+            key_back = [[-1, RESIDUES], [-RESIDUES, FOLDS]]
+            nc.gpsimd.memset(starts[:], float(REPEATS))
+            nc.gpsimd.affine_select(
+                out=starts[:], in_=starts[:], pattern=key, compare_op=ALU.is_equal, fill=0.0, base=0, channel_multiplier=-1
             )
+            nc.gpsimd.memset(run_mask[:], 0.0)
+            nc.gpsimd.memset(pick[:], 0.0)
+            nc.gpsimd.memset(run_pick[:], 0.0)
+            nc.gpsimd.memset(in_band[:], -1.0)
+            nc.gpsimd.affine_select(
+                out=in_band[:], in_=in_band[:], pattern=key, compare_op=ALU.is_ge, fill=0.0, base=0, channel_multiplier=-1
+            )
+            nc.gpsimd.affine_select(
+                out=in_band[:],
+                in_=in_band[:],
+                pattern=key_back,
+                compare_op=ALU.is_ge,
+                fill=0.0,
+                base=BAND - 1,
+                channel_multiplier=1,
+            )
+            make_identity(nc, ident_bf[:])
+            nc.gpsimd.memset(k_run[0:1, 0:NB, :], 0.0)
+
+        def setup_turn():
+            nc.vector.tensor_reduce(out=turn[:], in_=starts[:], axis=AXIS.X, op=ALU.add)
 
         def setup_band():
-            nc.vector.tensor_reduce(
-                out=turn[:],
-                in_=in_band[:].rearrange("p r a -> p (r a)").rearrange("p (a r) -> p r a", r=RESIDUES),
-                axis=AXIS.X,
-                op=ALU.add,
-            )
-            nc.vector.tensor_copy(out=in_band[:], in_=band[:].rearrange("p (a r) -> p r a", r=RESIDUES))
             both = banded[:].rearrange("p c n r a -> p (c n) r a")
             for low, high, start in ((0, RESIDUES - 1, 1), (RESIDUES - 1, RESIDUES, 0)):
                 shape = [P, 2 * TILES, high - low]
@@ -195,11 +197,6 @@ def tile_crosssliceattention_pa_kernel(tc, x, Wq_words, Wq_scales, bq, k_proj, o
                     in0=turn[:, start : start + high - low].unsqueeze(1).to_broadcast(shape),
                     scalar1=-MASKED,
                 )
-            for picks, places, count in ((pick, place, GATHER), (run_pick, run_place, RUN_GATHER)):
-                by_row = ident[:].rearrange("p (r e) -> p r e", e=count)
-                nc.vector.tensor_reduce(out=picks[:, 0 : P // count], in_=by_row, axis=AXIS.X, op=ALU.add)
-                by_place = ident[:].rearrange("p (r e) -> p e r", e=count)
-                nc.vector.tensor_reduce(out=places[:], in_=by_place, axis=AXIS.X, op=ALU.add)
             for i in range(NB):
                 for t in range(NB - i):
                     for n, m, w in ((0, i, i + t), (TILES - 1, P - 1 - i, P - 1 - i + BAND - 1 - t)):
@@ -212,6 +209,13 @@ def tile_crosssliceattention_pa_kernel(tc, x, Wq_words, Wq_scales, bq, k_proj, o
                             op0=ALU.mult,
                             op1=ALU.add,
                         )
+
+        def setup_picks():
+            for picks, places, count in ((pick, place, GATHER), (run_pick, run_place, RUN_GATHER)):
+                by_row = ident[:].rearrange("p (r e) -> p r e", e=count)
+                nc.vector.tensor_reduce(out=picks[:, 0 : P // count], in_=by_row, axis=AXIS.X, op=ALU.add)
+                by_place = ident[:].rearrange("p (r e) -> p e r", e=count)
+                nc.vector.tensor_reduce(out=places[:], in_=by_place, axis=AXIS.X, op=ALU.add)
 
         def setup_run_mask():
             for t in range(P * RUN):
@@ -229,11 +233,13 @@ def tile_crosssliceattention_pa_kernel(tc, x, Wq_words, Wq_scales, bq, k_proj, o
                         op1=ALU.add,
                     )
 
-        def bias_column():
+        def bias_column_scale():
             nc.vector.tensor_scalar_mul(out=bias_rows[0:CHUNKS, :], in0=bias_raw[:], scalar1=SCORE_SCALE)
+
+        def bias_column():
             bias_ps = psum.tile([P, P], F32, tag="bank")
             nc.tensor.transpose(bias_ps[:], bias_rows[:], ident[:])
-            nc.vector.tensor_copy(out=bias_col[:], in_=bias_ps[:, 0:CHUNKS])
+            nc.scalar.copy(out=bias_col[:], in_=bias_ps[:, 0:CHUNKS])
 
         def bias_row(h):
             wide_ps = psum.tile([P, BANK], F32, tag="bank")
@@ -604,21 +610,38 @@ def tile_crosssliceattention_pa_kernel(tc, x, Wq_words, Wq_scales, bq, k_proj, o
             for c in range(CHUNKS):
                 project_chunk(qT, codes, planes, blocks, c, "scalar" if c % 2 == 0 else EVEN_ENGINE)
 
-        setup_gpsimd()
-        setup_pads()
-        run_quantise(0, run_transpose(0))
-        for h in range(HALVES):
-            bias_row(h)
-        for i in range(1, RUN):
+        def head(i):
             run_quantise(i, run_transpose(i))
-        bias_column()
-        for h in range(HALVES):
-            for i in range(RUN):
+
+        def project_run(i):
+            for h in range(HALVES):
                 run_project(i, h)
-        setup_run_mask()
+
         first, blocks = groups[0]
-        codes, planes = prepare_x(first, blocks, [sort_x(groups[0], m, None) for m in range(blocks)])
-        setup_band()
+        with tc.manual_schedule():
+            setup_gpsimd()
+            setup_pads()
+            setup_turn()
+            setup_run_mask()
+            setup_picks()
+            bias_column_scale()
+            setup_band()
+            head(0)
+            head(1)
+            for h in range(HALVES):
+                bias_row(h)
+            bias_column()
+            project_run(0)
+            head(2)
+            head(3)
+            project_run(1)
+            project_run(2)
+            head(4)
+            head(5)
+            project_run(3)
+            project_run(4)
+            codes, planes = prepare_x(first, blocks, [sort_x(groups[0], m, None) for m in range(blocks)])
+            project_run(5)
         kT = kT_even
         if halo_block:
             transpose_keys(kT, first, -1)
@@ -626,7 +649,8 @@ def tile_crosssliceattention_pa_kernel(tc, x, Wq_words, Wq_scales, bq, k_proj, o
             transpose_keys(kT, first, m)
         qT = new_queries()
         project(qT, codes, planes, blocks)
-        sorts = [sort_x(groups[1], m, None) for m in range(groups[1][1])]
+        next_operands = prepare_x(groups[1][0], groups[1][1], [None] * groups[1][1])
+        sorts = []
         done = products(0, PRODUCTS_HEAD)
         served = 0
         run_served = 0
@@ -634,7 +658,7 @@ def tile_crosssliceattention_pa_kernel(tc, x, Wq_words, Wq_scales, bq, k_proj, o
             following = groups[index + 1] if index + 1 < len(groups) else None
             later = groups[index + 2] if index + 2 < len(groups) else None
             if following:
-                codes, planes = prepare_x(following[0], following[1], sorts)
+                codes, planes = next_operands if index == 0 else prepare_x(following[0], following[1], sorts)
                 sorts = []
                 next_kT = (kT_even, kT_odd)[(index + 1) % 2]
                 next_qT = new_queries()

@@ -126,17 +126,21 @@ def tile_crosssliceattention_pa_kernel(tc, x, Wq_words, Wq_scales, bq, k_proj, o
         load_w(1)
         for i in range(2, RUN):
             load_x_run(i)
-        for index, (first, blocks) in enumerate(groups):
+        first, blocks = groups[0]
+        for m in range(blocks):
+            load_x(first + m)
+        load_k(first - 1, blocks + 1)
+        load_k_run_own(0, RUN)
+        first, blocks = groups[1]
+        for m in range(blocks):
+            load_x(first + m)
+        load_k_run_left()
+        load_k_run_right()
+        load_k(*groups[1])
+        for first, blocks in groups[2:]:
             for m in range(blocks):
                 load_x(first + m)
-            if index == 0 and halo_block:
-                load_k(first - 1, blocks + 1)
-            else:
-                load_k(first, blocks)
-            if index == 0:
-                load_k_run_left()
-                load_k_run_own(0, RUN)
-                load_k_run_right()
+            load_k(first, blocks)
 
         ident = keep.tile([P, P], F32)
         ident_bf = keep.tile([P, P], BF16)
@@ -266,7 +270,11 @@ def tile_crosssliceattention_pa_kernel(tc, x, Wq_words, Wq_scales, bq, k_proj, o
                         nc.tensor.transpose(xT[:, g, u, :], sort[:, g, u, :], ident[:])
             return xT
 
-        def sort_words(tokens, engine, place):
+        sorted_tiles = []
+
+        def sort_words(tokens, engine):
+            place = len(sorted_tiles) % RUN
+            sorted_tiles.append(place)
             x_sorted = x_run[:, place, :].bitcast(F32).rearrange("t (g u p) -> t g u p", g=PASSES, u=2)
             copy_out(engine, x_sorted, tokens.bitcast(F32).rearrange("t (g p u) -> t g u p", g=PASSES, u=2))
             return x_sorted
@@ -578,7 +586,8 @@ def tile_crosssliceattention_pa_kernel(tc, x, Wq_words, Wq_scales, bq, k_proj, o
 
             return [lambda: (fold(), lowest()), exps, lambda: (turn_back(), invert(), weigh(), spread_out()), store]
 
-        units = [(i, j) for i in range(RUN) for j in range(BAND)]
+        order = sorted(range(RUN), key=lambda i: abs(2 * i - RUN + 1))
+        units = [(i, j) for i in order for j in range(BAND)]
         links = []
         run_links = []
 
@@ -592,8 +601,11 @@ def tile_crosssliceattention_pa_kernel(tc, x, Wq_words, Wq_scales, bq, k_proj, o
         def share_of(total, parts, index):
             return range(total * index // parts, total * (index + 1) // parts)
 
-        def sort_x(group, m, engine):
-            return sort_words(x_sb[:, group[0] + m - RUN, :], engine, (group[0] + m) % RUN) if engine else None
+        def sort_x(group, m):
+            return sort_words(x_sb[:, group[0] + m - RUN, :], "scalar")
+
+        def sort_run(i):
+            return sort_words(x_run[:, i, :], "scalar")
 
         def prepare_x(first, blocks, sorts):
             grouped = new_x()
@@ -610,8 +622,8 @@ def tile_crosssliceattention_pa_kernel(tc, x, Wq_words, Wq_scales, bq, k_proj, o
             for c in range(CHUNKS):
                 project_chunk(qT, codes, planes, blocks, c, "scalar" if c % 2 == 0 else EVEN_ENGINE)
 
-        def head(i):
-            run_quantise(i, run_transpose(i))
+        def head(i, sort=None):
+            run_quantise(i, run_transpose(i, "scalar", sort))
 
         def project_run(i):
             for h in range(HALVES):
@@ -632,64 +644,97 @@ def tile_crosssliceattention_pa_kernel(tc, x, Wq_words, Wq_scales, bq, k_proj, o
                 bias_row(h)
             bias_column()
             project_run(0)
+            sorts = [sort_run(3)]
             head(2)
-            head(3)
+            head(3, sorts[0])
+            sorts = [sort_run(4), sort_run(5)]
             project_run(1)
             project_run(2)
-            head(4)
-            head(5)
+            head(4, sorts[0])
+            head(5, sorts[1])
+            sorts = [None, sort_x(groups[0], 1)]
             project_run(3)
+            codes, planes = prepare_x(first, blocks, sorts)
+            second, second_blocks = groups[1]
             project_run(4)
-            codes, planes = prepare_x(first, blocks, [sort_x(groups[0], m, None) for m in range(blocks)])
-            project_run(5)
-        kT = kT_even
-        if halo_block:
+            kT = kT_even
             transpose_keys(kT, first, -1)
-        for m in range(blocks):
-            transpose_keys(kT, first, m)
-        qT = new_queries()
-        project(qT, codes, planes, blocks)
-        next_operands = prepare_x(groups[1][0], groups[1][1], [None] * groups[1][1])
-        sorts = []
-        done = products(0, PRODUCTS_HEAD)
-        served = 0
-        run_served = 0
-        for index, (first, blocks) in enumerate(groups):
-            following = groups[index + 1] if index + 1 < len(groups) else None
-            later = groups[index + 2] if index + 2 < len(groups) else None
-            if following:
-                codes, planes = next_operands if index == 0 else prepare_x(following[0], following[1], sorts)
-                sorts = []
-                next_kT = (kT_even, kT_odd)[(index + 1) % 2]
-                next_qT = new_queries()
-            for m in range(blocks):
-                if following and m == blocks - 1:
-                    project(next_qT, codes, planes, following[1])
+            transpose_keys(kT, first, 0)
+            project_run(5)
+            transpose_keys(kT, first, 1)
+            grouped = new_x()
+            next_operands = new_codes()
+            transpose_x(grouped, second, second_blocks, 0)
+            qT = new_queries()
+            done = products(0, 1)
+            project(qT, codes, planes, blocks)
+            transpose_x(grouped, second, second_blocks, 1)
+            transpose_x(grouped, second, second_blocks, 2)
+            done = products(done, 2)
+        third, third_blocks = groups[2]
+        with tc.manual_schedule(engines={mybir.EngineType.PE}):
+            def block_step(qT, kT, first, m, count):
                 block = band_block(qT, kT, first, m)
-                done = products(done, PRODUCTS_PER_BLOCK)
                 band_mask(block, first, m)
-                if served < len(links):
-                    links[served]()
-                    served += 1
-                if run_served < len(run_links):
-                    run_links[run_served]()
-                    run_served += 1
-                if following:
-                    for n in share_of(following[1], blocks, m):
-                        transpose_keys(next_kT, following[0], n)
-                elif m == blocks - 2:
-                    early = band_chain(first, blocks - 1)
-                    early[0]()
-                    early[1]()
-                if later:
-                    sorts.extend([sort_x(later, n, "scalar") for n in share_of(later[1], blocks, m)])
-            if following:
-                kT = next_kT
-                qT = next_qT
-                links.extend(band_chain(first, blocks))
-            else:
-                late = band_chain(first + blocks - 1, 1)
-                links.extend([late[0], late[1], early[2], late[2], early[3], late[3]])
-        done = products(done, len(units))
-        for link in run_links[run_served:] + links[served:]:
-            link()
+                return products(done, count)
+
+            block = band_block(qT, kT, first, 0)
+            transpose_x(grouped, second, second_blocks, 3)
+            quantise(grouped, *next_operands, second_blocks)
+            band_mask(block, first, 0)
+            kT_second = kT_odd
+            transpose_keys(kT_second, second, 0)
+            done = products(done, 3)
+            done = block_step(qT, kT, first, 1, 3)
+            transpose_keys(kT_second, second, 1)
+            transpose_keys(kT_second, second, 2)
+            qT_second = new_queries()
+            project(qT_second, *next_operands, second_blocks)
+            sorts = [sort_x(groups[2], n) for n in range(third_blocks)]
+            chain_first = band_chain(first, blocks)
+            chain_first[0]()
+            chain_first[1]()
+            transpose_keys(kT_second, second, 3)
+            done = block_step(qT_second, kT_second, second, 0, 3)
+            grouped = new_x()
+            codes, planes = new_codes()
+            transpose_x(grouped, third, third_blocks, 0, "scalar", sorts[0])
+            transpose_x(grouped, third, third_blocks, 1, "scalar", sorts[1])
+            chain_first[2]()
+            done = block_step(qT_second, kT_second, second, 1, 3)
+            transpose_x(grouped, third, third_blocks, 2, "scalar", sorts[2])
+            transpose_x(grouped, third, third_blocks, 3, "scalar", sorts[3])
+            quantise(grouped, codes, planes, third_blocks)
+            done = block_step(qT_second, kT_second, second, 2, 3)
+            chain_first[3]()
+            kT_third = kT_even
+            transpose_keys(kT_third, third, 0)
+            transpose_keys(kT_third, third, 1)
+            done = block_step(qT_second, kT_second, second, 3, 4)
+            transpose_keys(kT_third, third, 2)
+            qT_third = new_queries()
+            project(qT_third, codes, planes, third_blocks)
+            transpose_keys(kT_third, third, 3)
+            chain_second = band_chain(second, second_blocks)
+            chain_second[0]()
+            chain_second[1]()
+            done = block_step(qT_third, kT_third, third, 0, 4)
+            chain_second[2]()
+            done = block_step(qT_third, kT_third, third, 1, 4)
+            done = block_step(qT_third, kT_third, third, 2, len(units))
+            early = band_chain(third, third_blocks - 1)
+            early[0]()
+            early[1]()
+            block = band_block(qT_third, kT_third, third, third_blocks - 1)
+            for link in run_links[0:3]:
+                link()
+            early[2]()
+            band_mask(block, third, third_blocks - 1)
+            late = band_chain(third + third_blocks - 1, 1)
+            late[0]()
+            late[1]()
+            chain_second[3]()
+            run_links[3]()
+            early[3]()
+            late[2]()
+            late[3]()

@@ -38,6 +38,7 @@ REPEATS = RESIDUES + 1
 GATHER = 8
 RUN_GATHER = 4
 SCORE_SCALE = 1.0 / math.sqrt(D)
+OUTSIDE = 2.0**99
 MASKED = -1.0e30
 HALO_CUT = 112
 SORT_BUFS = 8
@@ -46,7 +47,6 @@ PRODUCTS_HEAD = 8
 PRODUCTS_PER_BLOCK = 3
 LAST_ALONE = False
 LINKS_PER_BLOCK = 2
-EVEN_ENGINE = "scalar"
 
 FLOPS = 2 * BATCHES * SEQ * D * D + 2 * BATCHES * SEQ * BAND * D
 
@@ -130,10 +130,10 @@ def tile_crosssliceattention_pa_kernel(tc, x, Wq_words, Wq_scales, bq, k_proj, o
         for m in range(blocks):
             load_x(first + m)
         load_k(first - 1, blocks + 1)
-        load_k_run_own(0, RUN)
         first, blocks = groups[1]
         for m in range(blocks):
             load_x(first + m)
+        load_k_run_own(0, RUN)
         load_k_run_left()
         load_k_run_right()
         load_k(*groups[1])
@@ -154,6 +154,7 @@ def tile_crosssliceattention_pa_kernel(tc, x, Wq_words, Wq_scales, bq, k_proj, o
         banded = keep.tile([P, 2, TILES, RESIDUES, RUN_COLUMNS], F32)
         starts = keep.tile([P, RESIDUES, FOLDS], F32)
         turn = keep.tile([P, RESIDUES], F32)
+        outside = keep.tile([P, WINDOW], BF16)
         bias_rows = keep.tile([P, P], F32)
         bias_col = keep.tile([P, CHUNKS], F32)
         bias_wide = keep.tile([P, D], F32)
@@ -173,7 +174,7 @@ def tile_crosssliceattention_pa_kernel(tc, x, Wq_words, Wq_scales, bq, k_proj, o
             nc.gpsimd.memset(run_mask[:], 0.0)
             nc.gpsimd.memset(pick[:], 0.0)
             nc.gpsimd.memset(run_pick[:], 0.0)
-            nc.gpsimd.memset(in_band[:], -1.0)
+            nc.gpsimd.memset(in_band[:], 1.0)
             nc.gpsimd.affine_select(
                 out=in_band[:], in_=in_band[:], pattern=key, compare_op=ALU.is_ge, fill=0.0, base=0, channel_multiplier=-1
             )
@@ -187,6 +188,18 @@ def tile_crosssliceattention_pa_kernel(tc, x, Wq_words, Wq_scales, bq, k_proj, o
                 channel_multiplier=1,
             )
             make_identity(nc, ident_bf[:])
+            nc.gpsimd.memset(outside[:], 0.0)
+            for step, base in ((1, 0), (-1, BAND - 1)):
+                nc.gpsimd.affine_select(
+                    out=outside[:],
+                    in_=outside[:],
+                    pattern=[[step, WINDOW]],
+                    compare_op=ALU.is_ge,
+                    fill=OUTSIDE,
+                    base=base,
+                    channel_multiplier=-step,
+                )
+            nc.gpsimd.memset(outside[:, WINDOW - NB : WINDOW], OUTSIDE)
             nc.gpsimd.memset(k_run[0:1, 0:NB, :], 0.0)
 
         def setup_turn():
@@ -238,7 +251,7 @@ def tile_crosssliceattention_pa_kernel(tc, x, Wq_words, Wq_scales, bq, k_proj, o
                     )
 
         def bias_column_scale():
-            nc.vector.tensor_scalar_mul(out=bias_rows[0:CHUNKS, :], in0=bias_raw[:], scalar1=SCORE_SCALE)
+            nc.vector.tensor_scalar_mul(out=bias_rows[0:CHUNKS, :], in0=bias_raw[:], scalar1=-SCORE_SCALE)
 
         def bias_column():
             bias_ps = psum.tile([P, P], F32, tag="bank")
@@ -339,9 +352,15 @@ def tile_crosssliceattention_pa_kernel(tc, x, Wq_words, Wq_scales, bq, k_proj, o
             run_spread = work.tile([P, RUN_GATHER, RUN * BAND], F32)
             run_gathered = work.tile([P, RUN_GATHER * RUN * BAND], F32)
 
-            def shift():
+            shape = [P, RUN_GATHER, RUN * BAND]
+
+            def mask():
                 nc.vector.tensor_add(out=run_scores[:], in0=run_scores[:], in1=run_mask[:])
+
+            def highest():
                 nc.vector.tensor_reduce(out=top[:], in_=run_scores[:], axis=AXIS.X, op=ALU.max)
+
+            def shift():
                 nc.vector.tensor_sub(
                     out=run_scores[:], in0=run_scores[:], in1=top[:].unsqueeze(2).to_broadcast(rows + [BAND])
                 )
@@ -349,13 +368,18 @@ def tile_crosssliceattention_pa_kernel(tc, x, Wq_words, Wq_scales, bq, k_proj, o
             def exps():
                 nc.scalar.activation(out=run_weights[:], in_=run_scores[:], func=ACT.Exp)
 
-            def divide():
+            def sums():
                 nc.vector.tensor_reduce(out=run_total[:], in_=run_weights[:], axis=AXIS.X, op=ALU.add)
+
+            def invert():
                 nc.vector.reciprocal(out=run_total[:], in_=run_total[:])
+
+            def divide():
                 nc.vector.tensor_mul(
                     out=run_weights[:], in0=run_weights[:], in1=run_total[:].unsqueeze(2).to_broadcast(rows + [BAND])
                 )
-                shape = [P, RUN_GATHER, RUN * BAND]
+
+            def spread_out():
                 nc.vector.tensor_mul(
                     out=run_spread[:],
                     in0=run_weights[:].rearrange("p i j -> p (i j)").unsqueeze(1).to_broadcast(shape),
@@ -373,12 +397,12 @@ def tile_crosssliceattention_pa_kernel(tc, x, Wq_words, Wq_scales, bq, k_proj, o
                 )
                 runs = P // RUN_GATHER
                 nc.scalar.copy(out=run_gathered[0:runs, :], in_=run_ps[0:runs, :])
-                nc.scalar.dma_start(
+                nc.sync.dma_start(
                     out=out_rows[0 : P * RUN].rearrange("(m e i) j -> m (e i j)", e=RUN_GATHER, i=RUN),
                     in_=run_gathered[0:runs, :],
                 )
 
-            return [shift, exps, divide, store]
+            return [mask, highest, shift, exps, sums, invert, divide, spread_out, store]
 
         def new_x():
             grouped = work.tile([P, PASSES, SEQ, PACK], BF16, align_bytes=64)
@@ -418,7 +442,7 @@ def tile_crosssliceattention_pa_kernel(tc, x, Wq_words, Wq_scales, bq, k_proj, o
             qT = work.tile([P, CHUNKS, SEQ], F32)
             return qT
 
-        def project_chunk(qT, codes, planes, blocks, c, engine="scalar"):
+        def project_chunk(qT, codes, planes, blocks, c):
             acc = psum.tile([P, SEQ], F32, tag="bank")
             flat_codes = codes[:].rearrange("p g m -> p (g m)")
             flat_planes = planes[:].rearrange("p g m -> p (g m)")
@@ -440,23 +464,13 @@ def tile_crosssliceattention_pa_kernel(tc, x, Wq_words, Wq_scales, bq, k_proj, o
                         start=(g == 0),
                         stop=(g == PASSES - 1),
                     )
-            if engine == "scalar":
-                nc.scalar.activation(
-                    out=qT[:, c, 0 : P * blocks],
-                    in_=acc[:, 0 : P * blocks],
-                    func=ACT.Identity,
-                    bias=bias_col[:, c : c + 1],
-                    scale=SCORE_SCALE,
-                )
-            else:
-                nc.vector.tensor_scalar(
-                    out=qT[:, c, 0 : P * blocks],
-                    in0=acc[:, 0 : P * blocks],
-                    scalar1=SCORE_SCALE,
-                    scalar2=bias_col[:, c : c + 1],
-                    op0=ALU.mult,
-                    op1=ALU.add,
-                )
+            nc.scalar.activation(
+                out=qT[:, c, 0 : P * blocks],
+                in_=acc[:, 0 : P * blocks],
+                func=ACT.Identity,
+                bias=bias_col[:, c : c + 1],
+                scale=-SCORE_SCALE,
+            )
 
         kT_even = keep.tile([P, CHUNKS, PAD + SEQ + PAD], F32)
         kT_odd = keep.tile([P, CHUNKS, PAD + SEQ + PAD], F32)
@@ -478,15 +492,17 @@ def tile_crosssliceattention_pa_kernel(tc, x, Wq_words, Wq_scales, bq, k_proj, o
             else:
                 copy_out(engine, kT[:, :, PAD + P * m : PAD + P * (m + 1)], kT_ps[:])
 
-        def band_block(qT, kT, first, m):
+        def band_block(qT, kT, first, m, masked=False):
             block = psum.tile([P, WINDOW], F32, tag="bank")
             first_key = PAD - NB + P * m
+            if masked:
+                nc.tensor.matmul(out=block[:], lhsT=ident_bf[:], rhs=outside[:], start=True, stop=False)
             for c in range(CHUNKS):
                 nc.tensor.matmul(
                     out=block[:],
                     lhsT=qT[:, c, P * m : P * (m + 1)],
                     rhs=kT[:, c, first_key : first_key + WINDOW],
-                    start=(c == 0),
+                    start=(c == 0 and not masked),
                     stop=(c == CHUNKS - 1),
                 )
             return block
@@ -499,7 +515,7 @@ def tile_crosssliceattention_pa_kernel(tc, x, Wq_words, Wq_scales, bq, k_proj, o
                 in1=in_band[:],
             )
 
-        def band_chain(first, blocks):
+        def band_chain(first, blocks, block=None):
             lo = first % TILES
             folded = work.tile([P, TILES, RESIDUES], F32)
             low = work.tile([P, TILES], F32)
@@ -510,6 +526,11 @@ def tile_crosssliceattention_pa_kernel(tc, x, Wq_words, Wq_scales, bq, k_proj, o
             weights = work.tile([P, TILES, BAND], F32)
             spread = work.tile([P, TILES, GATHER, BAND], F32)
             gathered = work.tile([P, TILES, GATHER, BAND], F32)
+
+            def fold_masked():
+                nc.vector.tensor_reduce(out=low[:, 0:1], in_=block[:], axis=AXIS.X, op=ALU.min)
+                by_residue = block[:].rearrange("p (a r) -> p r a", r=RESIDUES)
+                nc.vector.tensor_reduce(out=folded[:, 0, :], in_=by_residue, axis=AXIS.X, op=ALU.min)
 
             def fold():
                 nc.vector.tensor_reduce(
@@ -535,6 +556,8 @@ def tile_crosssliceattention_pa_kernel(tc, x, Wq_words, Wq_scales, bq, k_proj, o
 
             def invert():
                 nc.vector.reciprocal(out=total[:, 0:blocks], in_=total[:, 0:blocks])
+
+            def shares():
                 nc.vector.tensor_mul(
                     out=share[:, 0:blocks, :],
                     in0=place[:].unsqueeze(1).to_broadcast([P, blocks, GATHER]),
@@ -579,12 +602,15 @@ def tile_crosssliceattention_pa_kernel(tc, x, Wq_words, Wq_scales, bq, k_proj, o
                     out=gathered[0:rows, 0:blocks].rearrange("p n e j -> p (n e j)"),
                     in_=gathered_ps[0:rows, 0:blocks].rearrange("p n c -> p (n c)"),
                 )
-                nc.scalar.dma_start(
+                store_queue = nc.sync if block is None else nc.scalar
+                store_queue.dma_start(
                     out=out_rows[P * first : P * (first + blocks)].rearrange("(n m e) j -> m n (e j)", m=rows, e=GATHER),
                     in_=gathered[0:rows, 0:blocks].rearrange("m n e j -> m n (e j)"),
                 )
 
-            return [lambda: (fold(), lowest()), exps, lambda: (turn_back(), invert(), weigh(), spread_out()), store]
+            if block is not None:
+                return [fold_masked, exps, turn_back, invert, shares, weigh, spread_out, store]
+            return [fold, lowest, exps, turn_back, invert, shares, weigh, spread_out, store]
 
         order = sorted(range(RUN), key=lambda i: abs(2 * i - RUN + 1))
         units = [(i, j) for i in order for j in range(BAND)]
@@ -618,9 +644,9 @@ def tile_crosssliceattention_pa_kernel(tc, x, Wq_words, Wq_scales, bq, k_proj, o
                 quantise(grouped, codes, planes, blocks)
             return codes, planes
 
-        def project(qT, codes, planes, blocks):
-            for c in range(CHUNKS):
-                project_chunk(qT, codes, planes, blocks, c, "scalar" if c % 2 == 0 else EVEN_ENGINE)
+        def project(qT, codes, planes, blocks, chunks=range(CHUNKS)):
+            for c in chunks:
+                project_chunk(qT, codes, planes, blocks, c)
 
         def head(i, sort=None):
             run_quantise(i, run_transpose(i, "scalar", sort))
@@ -628,6 +654,13 @@ def tile_crosssliceattention_pa_kernel(tc, x, Wq_words, Wq_scales, bq, k_proj, o
         def project_run(i):
             for h in range(HALVES):
                 run_project(i, h)
+
+        filled = []
+
+        def fill(count):
+            for i, j in units[len(filled) : len(filled) + count]:
+                run_product(i, j)
+                filled.append((i, j))
 
         first, blocks = groups[0]
         with tc.manual_schedule():
@@ -658,83 +691,132 @@ def tile_crosssliceattention_pa_kernel(tc, x, Wq_words, Wq_scales, bq, k_proj, o
             second, second_blocks = groups[1]
             project_run(4)
             kT = kT_even
+            sorts = [sort_x(groups[1], 0)]
             transpose_keys(kT, first, -1)
             transpose_keys(kT, first, 0)
+            sorts.append(sort_x(groups[1], 1))
             project_run(5)
             transpose_keys(kT, first, 1)
             grouped = new_x()
             next_operands = new_codes()
-            transpose_x(grouped, second, second_blocks, 0)
+            transpose_x(grouped, second, second_blocks, 0, "scalar", sorts[0])
+            transpose_x(grouped, second, second_blocks, 1, "scalar", sorts[1])
             qT = new_queries()
-            done = products(0, 1)
+            fill(1)
             project(qT, codes, planes, blocks)
-            transpose_x(grouped, second, second_blocks, 1)
             transpose_x(grouped, second, second_blocks, 2)
-            done = products(done, 2)
-        third, third_blocks = groups[2]
-        with tc.manual_schedule(engines={mybir.EngineType.PE}):
-            def block_step(qT, kT, first, m, count):
-                block = band_block(qT, kT, first, m)
-                band_mask(block, first, m)
-                return products(done, count)
-
-            block = band_block(qT, kT, first, 0)
             transpose_x(grouped, second, second_blocks, 3)
+            fill(4)
             quantise(grouped, *next_operands, second_blocks)
-            band_mask(block, first, 0)
+
+            third, third_blocks = groups[2]
             kT_second = kT_odd
+            qT_second = new_queries()
+            block = band_block(qT, kT, first, 0)
             transpose_keys(kT_second, second, 0)
-            done = products(done, 3)
-            done = block_step(qT, kT, first, 1, 3)
+            band_mask(block, first, 0)
+            fill(2)
+            block = band_block(qT, kT, first, 1)
             transpose_keys(kT_second, second, 1)
             transpose_keys(kT_second, second, 2)
-            qT_second = new_queries()
-            project(qT_second, *next_operands, second_blocks)
-            sorts = [sort_x(groups[2], n) for n in range(third_blocks)]
-            chain_first = band_chain(first, blocks)
-            chain_first[0]()
-            chain_first[1]()
+            band_mask(block, first, 1)
+            chain = band_chain(first, blocks)
+            chain[0]()
+            fill(1)
+            chain[1]()
+            project(qT_second, *next_operands, second_blocks, range(0, 4))
+            chain[2]()
+            project(qT_second, *next_operands, second_blocks, range(4, 8))
+            sorts = [sort_x(groups[2], n) for n in range(2)]
             transpose_keys(kT_second, second, 3)
-            done = block_step(qT_second, kT_second, second, 0, 3)
+            fill(3)
+            chain[3]()
+            fill(1)
+            chain[4]()
+            fill(1)
+            chain[5]()
+
             grouped = new_x()
             codes, planes = new_codes()
+            qT_third = new_queries()
+            kT_third = kT_even
+            block = band_block(qT_second, kT_second, second, 0)
             transpose_x(grouped, third, third_blocks, 0, "scalar", sorts[0])
             transpose_x(grouped, third, third_blocks, 1, "scalar", sorts[1])
-            chain_first[2]()
-            done = block_step(qT_second, kT_second, second, 1, 3)
+            sorts.extend([sort_x(groups[2], n) for n in range(2, 4)])
+            chain[6]()
+            band_mask(block, second, 0)
+            chain[7]()
+            block = band_block(qT_second, kT_second, second, 1)
             transpose_x(grouped, third, third_blocks, 2, "scalar", sorts[2])
             transpose_x(grouped, third, third_blocks, 3, "scalar", sorts[3])
-            quantise(grouped, codes, planes, third_blocks)
-            done = block_step(qT_second, kT_second, second, 2, 3)
-            chain_first[3]()
-            kT_third = kT_even
+            fill(3)
+            band_mask(block, second, 1)
+            block = band_block(qT_second, kT_second, second, 2)
+            chain[8]()
             transpose_keys(kT_third, third, 0)
             transpose_keys(kT_third, third, 1)
-            done = block_step(qT_second, kT_second, second, 3, 4)
+            fill(2)
+            quantise(grouped, codes, planes, third_blocks)
+            band_mask(block, second, 2)
+            fill(2)
+            block = band_block(qT_second, kT_second, second, 3)
             transpose_keys(kT_third, third, 2)
-            qT_third = new_queries()
-            project(qT_third, codes, planes, third_blocks)
+            band_mask(block, second, 3)
+            chain = band_chain(second, second_blocks)
+            chain[0]()
+            fill(1)
+            chain[1]()
+            project(qT_third, codes, planes, third_blocks, range(0, 4))
+            chain[2]()
+            project(qT_third, codes, planes, third_blocks, range(4, 8))
             transpose_keys(kT_third, third, 3)
-            chain_second = band_chain(second, second_blocks)
-            chain_second[0]()
-            chain_second[1]()
-            done = block_step(qT_third, kT_third, third, 0, 4)
-            chain_second[2]()
-            done = block_step(qT_third, kT_third, third, 1, 4)
-            done = block_step(qT_third, kT_third, third, 2, len(units))
+            fill(3)
+            chain[3]()
+            fill(1)
+            chain[4]()
+
+            block = band_block(qT_third, kT_third, third, 0)
+            fill(1)
+            chain[5]()
+            fill(1)
+            chain[6]()
+            band_mask(block, third, 0)
+            chain[7]()
+            block = band_block(qT_third, kT_third, third, 1)
+            fill(2)
+            band_mask(block, third, 1)
+            fill(len(units))
+            run_links = run_chain()
+            block = band_block(qT_third, kT_third, third, 2)
+            band_mask(block, third, 2)
             early = band_chain(third, third_blocks - 1)
+            block = band_block(qT_third, kT_third, third, third_blocks - 1, masked=True)
+            late = band_chain(third + third_blocks - 1, 1, block)
+            run_links[0]()
             early[0]()
+            run_links[1]()
             early[1]()
-            block = band_block(qT_third, kT_third, third, third_blocks - 1)
-            for link in run_links[0:3]:
-                link()
+            run_links[2]()
             early[2]()
-            band_mask(block, third, third_blocks - 1)
-            late = band_chain(third + third_blocks - 1, 1)
+            run_links[3]()
             late[0]()
             late[1]()
-            chain_second[3]()
-            run_links[3]()
+            run_links[4]()
             early[3]()
+            run_links[5]()
+            early[4]()
             late[2]()
+            run_links[6]()
             late[3]()
+            early[5]()
+            late[5]()
+            late[4]()
+            early[6]()
+            run_links[7]()
+            late[6]()
+            early[7]()
+            chain[8]()
+            run_links[8]()
+            early[8]()
+            late[7]()

import math

import concourse.mybir as mybir
from concourse.masks import make_identity

BF16 = mybir.dt.bfloat16
F32 = mybir.dt.float32
I32 = mybir.dt.int32
U8 = mybir.dt.uint8
U32 = mybir.dt.uint32
FP8X4 = mybir.dt.float8_e4m3fn_x4
FP4X4 = mybir.dt.float4_e2m1fn_x4
ACT = mybir.ActivationFunctionType
ALU = mybir.AluOpType
AXIS = mybir.AxisListType

P = 128
BATCHES, SEQ, D = 4, 512, 1024
NB = 2
BAND = 2 * NB + 1
TILES = SEQ // P
BLOCKS = BATCHES * TILES
RUN = 6
SLOTS = RUN + 2 * NB
PACK = 4
K_PASS = P * PACK
PASSES = D // K_PASS
CHUNKS = D // P
BANK = 512
PSUM_BANKS = 8
HALVES = D // BANK
PAD = 8
WINDOW = P + 2 * NB
RESIDUES = BAND + 1
FOLDS = WINDOW // RESIDUES
RUN_COLUMNS = FOLDS + 2
REPEATS = RESIDUES + 1
GATHER = 8
RUN_GATHER = 4
SCORE_SCALE = 1.0 / math.sqrt(D)
OUTSIDE = 2.0**99
MASKED = -1.0e30
HALO_CUT = 112
SORT_BUFS = 8
SORT_ENGINE = "vector"
PRODUCTS_HEAD = 8
PRODUCTS_PER_BLOCK = 3
LAST_ALONE = False
LINKS_PER_BLOCK = 2

FLOPS = 2 * BATCHES * SEQ * D * D + 2 * BATCHES * SEQ * BAND * D


def tile_crosssliceattention_pa_kernel(tc, x, Wq_words, Wq_scales, bq, k_proj, out):
    nc = tc.nc
    x_rows = x.rearrange("b s k -> (b s) k")
    k_rows = k_proj.rearrange("b s d -> (b s) d")
    out_rows = out.rearrange("b s j -> (b s) j")
    groups = [(max(TILES * b, RUN), TILES * (b + 1) - max(TILES * b, RUN)) for b in range(BATCHES) if TILES * (b + 1) > RUN]
    halo_block = RUN % TILES != 0

    with tc.tile_pool(name="keep", bufs=1) as keep, tc.tile_pool(name="work", bufs=2) as work, tc.psum_pool(
        name="psum", bufs=PSUM_BANKS
    ) as psum:
        x_run = keep.tile([P, RUN, D], BF16)
        x_sb = keep.tile([P, BLOCKS - RUN, D], BF16)
        k_run = keep.tile([P, SLOTS, D], BF16)
        k_sb = keep.tile([P, BLOCKS - RUN + 1, D], BF16)
        w_words = keep.tile([P, PASSES, 2 * D], U8, align_bytes=64)
        w_planes = keep.tile([P, PASSES, D], U8, align_bytes=64)
        bias_raw = keep.tile([CHUNKS, P], BF16)
        bias_top = keep.tile([P, D], BF16)
        ones = keep.tile([P, P], BF16)

        nc.vector.memset(w_planes[:].bitcast(I32), 0)
        nc.vector.memset(bias_top[:], 0.0)

        def load_x_run(i):
            nc.sync.dma_start(out=x_run[:, i, :], in_=x_rows[0 : P * RUN].rearrange("(p i) k -> p i k", i=RUN)[:, i, :])

        def load_x(t):
            nc.sync.dma_start(out=x_sb[:, t - RUN, :], in_=x_rows[P * t : P * (t + 1)])

        def load_k(first, blocks):
            nc.sync.dma_start(
                out=k_sb[:, first - RUN + 1 : first - RUN + 1 + blocks, :],
                in_=k_rows[P * first : P * (first + blocks)].rearrange("(n p) d -> p n d", p=P),
            )

        def load_w(h):
            half = slice(2 * BANK * h, 2 * BANK * (h + 1))
            nc.sync.dma_start(
                out=w_words[:, :, half].bitcast(I32),
                in_=Wq_words.rearrange("g p b -> p g b")[:, :, half].bitcast(I32),
            )

        def load_scales():
            for quad in range(4):
                nc.sync.dma_start(
                    out=w_planes[32 * quad : 32 * quad + 4].bitcast(I32),
                    in_=Wq_scales[:, 4 * quad : 4 * quad + 4, :].rearrange("g r n -> r g n").bitcast(I32),
                )

        def load_k_run_own(first, last):
            nc.sync.dma_start(
                out=k_run[:, NB + first : NB + last, :],
                in_=k_rows[0 : P * RUN].rearrange("(p i) d -> p i d", i=RUN)[:, first:last, :],
            )

        def load_k_run_left():
            before = k_rows[RUN - NB : RUN - NB + (P - 1) * RUN].rearrange("(p i) d -> p i d", i=RUN)
            cut = P - HALO_CUT
            nc.sync.dma_start(out=k_run[1:cut, 0:NB, :], in_=before[0 : cut - 1, 0:NB, :])
            nc.sync.dma_start(out=k_run[cut:P, 0:NB, :], in_=before[cut - 1 : P - 1, 0:NB, :])

        def load_k_run_right():
            after = k_rows[RUN : RUN + P * RUN].rearrange("(p i) d -> p i d", i=RUN)
            nc.sync.dma_start(out=k_run[:, SLOTS - NB : SLOTS, :], in_=after[:, 0:NB, :])

        load_x_run(0)
        nc.sync.dma_start(out=bias_raw[:], in_=bq.rearrange("(c f) -> c f", f=P))
        nc.sync.dma_start(out=bias_top[0:1, :], in_=bq.rearrange("(o n) -> o n", o=1))
        load_x_run(1)
        load_scales()
        load_w(0)
        load_w(1)
        for i in range(2, RUN):
            load_x_run(i)
        first, blocks = groups[0]
        for m in range(blocks):
            load_x(first + m)
        load_k(first - 1, blocks + 1)
        first, blocks = groups[1]
        for m in range(blocks):
            load_x(first + m)
        load_k_run_own(0, RUN)
        load_k_run_left()
        load_k_run_right()
        load_k(*groups[1])
        for first, blocks in groups[2:]:
            for m in range(blocks):
                load_x(first + m)
            load_k(first, blocks)

        ident = keep.tile([P, P], F32)
        ident_bf = keep.tile([P, P], BF16)
        warm = keep.tile([P, 1], F32)
        pick = keep.tile([P, P], F32)
        place = keep.tile([P, GATHER], F32)
        run_pick = keep.tile([P, P], F32)
        run_place = keep.tile([P, RUN_GATHER], F32)
        run_mask = keep.tile([P, RUN, BAND], F32)
        in_band = keep.tile([P, RESIDUES, FOLDS], F32)
        banded = keep.tile([P, 2, TILES, RESIDUES, RUN_COLUMNS], F32)
        starts = keep.tile([P, RESIDUES, FOLDS], F32)
        turn = keep.tile([P, RESIDUES], F32)
        outside = keep.tile([P, WINDOW], BF16)
        bias_rows = keep.tile([P, P], F32)
        bias_col = keep.tile([P, CHUNKS], F32)
        bias_wide = keep.tile([P, D], F32)

        def setup_gpsimd():
            make_identity(nc, ident[:])
            nc.gpsimd.memset(warm[:], 0.0)
            nc.scalar.activation(out=warm[:], in_=warm[:], func=ACT.Exp)
            nc.gpsimd.memset(ones[:], 1.0)
            nc.gpsimd.memset(bias_rows[:], 0.0)
            key = [[1, RESIDUES], [RESIDUES, FOLDS]]
            key_back = [[-1, RESIDUES], [-RESIDUES, FOLDS]]
            nc.gpsimd.memset(starts[:], float(REPEATS))
            nc.gpsimd.affine_select(
                out=starts[:], in_=starts[:], pattern=key, compare_op=ALU.is_equal, fill=0.0, base=0, channel_multiplier=-1
            )
            nc.gpsimd.memset(run_mask[:], 0.0)
            nc.gpsimd.memset(pick[:], 0.0)
            nc.gpsimd.memset(run_pick[:], 0.0)
            nc.gpsimd.memset(in_band[:], 1.0)
            nc.gpsimd.affine_select(
                out=in_band[:], in_=in_band[:], pattern=key, compare_op=ALU.is_ge, fill=0.0, base=0, channel_multiplier=-1
            )
            nc.gpsimd.affine_select(
                out=in_band[:],
                in_=in_band[:],
                pattern=key_back,
                compare_op=ALU.is_ge,
                fill=0.0,
                base=BAND - 1,
                channel_multiplier=1,
            )
            make_identity(nc, ident_bf[:])
            nc.gpsimd.memset(outside[:], 0.0)
            for step, base in ((1, 0), (-1, BAND - 1)):
                nc.gpsimd.affine_select(
                    out=outside[:],
                    in_=outside[:],
                    pattern=[[step, WINDOW]],
                    compare_op=ALU.is_ge,
                    fill=OUTSIDE,
                    base=base,
                    channel_multiplier=-step,
                )
            nc.gpsimd.memset(outside[:, WINDOW - NB : WINDOW], OUTSIDE)
            nc.gpsimd.memset(k_run[0:1, 0:NB, :], 0.0)

        def setup_turn():
            nc.vector.tensor_reduce(out=turn[:], in_=starts[:], axis=AXIS.X, op=ALU.add)

        def setup_band():
            both = banded[:].rearrange("p c n r a -> p (c n) r a")
            for low, high, start in ((0, RESIDUES - 1, 1), (RESIDUES - 1, RESIDUES, 0)):
                shape = [P, 2 * TILES, high - low]
                nc.vector.tensor_scalar_mul(
                    out=both[:, :, low:high, FOLDS],
                    in0=turn[:, start : start + high - low].unsqueeze(1).to_broadcast(shape),
                    scalar1=-MASKED,
                )
            for i in range(NB):
                for t in range(NB - i):
                    for n, m, w in ((0, i, i + t), (TILES - 1, P - 1 - i, P - 1 - i + BAND - 1 - t)):
                        spot = (w % RESIDUES, FOLDS)
                        nc.vector.scalar_tensor_tensor(
                            out=banded[:, :, n, spot[0], spot[1]],
                            in0=ident[:, m : m + 1].to_broadcast([P, 2]),
                            scalar=-MASKED,
                            in1=banded[:, :, n, spot[0], spot[1]],
                            op0=ALU.mult,
                            op1=ALU.add,
                        )

        def setup_picks():
            for picks, places, count in ((pick, place, GATHER), (run_pick, run_place, RUN_GATHER)):
                by_row = ident[:].rearrange("p (r e) -> p r e", e=count)
                nc.vector.tensor_reduce(out=picks[:, 0 : P // count], in_=by_row, axis=AXIS.X, op=ALU.add)
                by_place = ident[:].rearrange("p (r e) -> p e r", e=count)
                nc.vector.tensor_reduce(out=places[:], in_=by_place, axis=AXIS.X, op=ALU.add)

        def setup_run_mask():
            for t in range(P * RUN):
                s = t % SEQ
                missing = max(NB - s, NB - (SEQ - 1 - s))
                if missing > 0:
                    first = 0 if s < NB else BAND - missing
                    columns = run_mask[:, t % RUN, first : first + missing]
                    nc.vector.scalar_tensor_tensor(
                        out=columns,
                        in0=ident[:, t // RUN : t // RUN + 1].to_broadcast([P, missing]),
                        scalar=MASKED,
                        in1=columns,
                        op0=ALU.mult,
                        op1=ALU.add,
                    )

        def bias_column_scale():
            nc.vector.tensor_scalar_mul(out=bias_rows[0:CHUNKS, :], in0=bias_raw[:], scalar1=-SCORE_SCALE)

        def bias_column():
            bias_ps = psum.tile([P, P], F32, tag="bank")
            nc.tensor.transpose(bias_ps[:], bias_rows[:], ident[:])
            nc.scalar.copy(out=bias_col[:], in_=bias_ps[:, 0:CHUNKS])

        def bias_row(h):
            wide_ps = psum.tile([P, BANK], F32, tag="bank")
            nc.tensor.matmul(
                out=wide_ps[:], lhsT=ones[:], rhs=bias_top[:, BANK * h : BANK * (h + 1)], start=True, stop=True
            )
            nc.scalar.mul(out=bias_wide[:, BANK * h : BANK * (h + 1)], in_=wide_ps[:], mul=SCORE_SCALE)

        def copy_out(engine, out_ap, in_ap):
            if engine == "scalar":
                nc.scalar.copy(out=out_ap, in_=in_ap)
            else:
                nc.vector.tensor_copy(out=out_ap, in_=in_ap)

        def transpose_words(tokens, sort):
            x_pairs = tokens.bitcast(F32)
            xT = psum.tile([P, PASSES, 2, P], F32, tag="bank")
            for g in range(PASSES):
                for u in range(2):
                    first = (K_PASS // 2) * g + u
                    if sort is None:
                        nc.tensor.transpose(xT[:, g, u, :], x_pairs[:, first : (K_PASS // 2) * (g + 1) : 2], ident[:])
                    else:
                        nc.tensor.transpose(xT[:, g, u, :], sort[:, g, u, :], ident[:])
            return xT

        sorted_tiles = []

        def sort_words(tokens, engine):
            place = len(sorted_tiles) % RUN
            sorted_tiles.append(place)
            x_sorted = x_run[:, place, :].bitcast(F32).rearrange("t (g u p) -> t g u p", g=PASSES, u=2)
            copy_out(engine, x_sorted, tokens.bitcast(F32).rearrange("t (g p u) -> t g u p", g=PASSES, u=2))
            return x_sorted

        q_run = keep.tile([P, RUN, D], F32)
        run_scores = keep.tile([P, RUN, BAND], F32)
        run_codes = keep.tile([P, RUN, PASSES, P], U32, align_bytes=64)
        run_planes = keep.tile([P, RUN, PASSES, P], U8, align_bytes=64)

        def run_transpose(i, engine="scalar", sort=None):
            xT = transpose_words(x_run[:, i, :], sort)
            run_grouped = work.tile([P, PASSES, P, PACK], BF16, align_bytes=64, bufs=3)
            copy_out(engine, run_grouped[:].bitcast(F32), xT[:].rearrange("p g u m -> p g m u"))
            return run_grouped

        def run_quantise(i, run_grouped):
            nc.vector.quantize_mx(
                out=run_codes[:, i].rearrange("p g m -> p (g m)").bitcast(FP8X4),
                scales=run_planes[:, i].rearrange("p g m -> p (g m)"),
                in_=run_grouped[:].rearrange("p g m t -> p (g m t)"),
            )

        def run_project(i, h):
            features = slice(BANK * h, BANK * (h + 1))
            acc = psum.tile([P, BANK], F32, tag="bank")
            for g in range(PASSES):
                nc.tensor.matmul_mx(
                    out=acc[:],
                    lhsT=run_codes[:, i, g, :].bitcast(FP8X4),
                    lhsT_scale=run_planes[:, i, g, :],
                    rhs=w_words[:, g, 2 * BANK * h : 2 * BANK * (h + 1)].bitcast(FP4X4),
                    rhs_scale=w_planes[:, g, features],
                    start=(g == 0),
                    stop=(g == PASSES - 1),
                )
            nc.vector.scalar_tensor_tensor(
                out=q_run[:, i, features],
                in0=acc[:],
                scalar=SCORE_SCALE,
                in1=bias_wide[:, features],
                op0=ALU.mult,
                op1=ALU.add,
            )

        def run_product(i, j):
            products = work.tile([P, D], F32, bufs=2)
            nc.vector.scalar_tensor_tensor(
                out=products[:],
                in0=q_run[:, i, :],
                scalar=1.0,
                in1=k_run[:, i + j, :],
                op0=ALU.mult,
                op1=ALU.mult,
                accum_out=run_scores[:, i, j : j + 1],
            )

        def run_chain():
            rows = [P, RUN]
            top = work.tile(rows, F32)
            run_weights = work.tile(rows + [BAND], F32)
            run_total = work.tile(rows, F32)
            run_spread = work.tile([P, RUN_GATHER, RUN * BAND], F32)
            run_gathered = work.tile([P, RUN_GATHER * RUN * BAND], F32)

            shape = [P, RUN_GATHER, RUN * BAND]

            def mask():
                nc.vector.tensor_add(out=run_scores[:], in0=run_scores[:], in1=run_mask[:])

            def highest():
                nc.vector.tensor_reduce(out=top[:], in_=run_scores[:], axis=AXIS.X, op=ALU.max)

            def shift():
                nc.vector.tensor_sub(
                    out=run_scores[:], in0=run_scores[:], in1=top[:].unsqueeze(2).to_broadcast(rows + [BAND])
                )

            def exps():
                nc.scalar.activation(out=run_weights[:], in_=run_scores[:], func=ACT.Exp)

            def sums():
                nc.vector.tensor_reduce(out=run_total[:], in_=run_weights[:], axis=AXIS.X, op=ALU.add)

            def invert():
                nc.vector.reciprocal(out=run_total[:], in_=run_total[:])

            def divide():
                nc.vector.tensor_mul(
                    out=run_weights[:], in0=run_weights[:], in1=run_total[:].unsqueeze(2).to_broadcast(rows + [BAND])
                )

            def spread_out():
                nc.vector.tensor_mul(
                    out=run_spread[:],
                    in0=run_weights[:].rearrange("p i j -> p (i j)").unsqueeze(1).to_broadcast(shape),
                    in1=run_place[:].unsqueeze(2).to_broadcast(shape),
                )

            def store():
                run_ps = psum.tile([P, RUN_GATHER * RUN * BAND], F32, tag="bank")
                nc.tensor.matmul(
                    out=run_ps[:],
                    lhsT=run_pick[:],
                    rhs=run_spread[:].rearrange("p e c -> p (e c)"),
                    start=True,
                    stop=True,
                )
                runs = P // RUN_GATHER
                nc.scalar.copy(out=run_gathered[0:runs, :], in_=run_ps[0:runs, :])
                nc.sync.dma_start(
                    out=out_rows[0 : P * RUN].rearrange("(m e i) j -> m (e i j)", e=RUN_GATHER, i=RUN),
                    in_=run_gathered[0:runs, :],
                )

            return [mask, highest, shift, exps, sums, invert, divide, spread_out, store]

        def new_x():
            grouped = work.tile([P, PASSES, SEQ, PACK], BF16, align_bytes=64)
            return grouped

        def transpose_x(grouped, first, blocks, m, engine="scalar", sort=None):
            xT = transpose_words(x_sb[:, first + m - RUN, :], sort)
            pairs = grouped[:].bitcast(F32)
            if blocks == TILES:
                copy_out(engine, pairs[:, :, P * m : P * (m + 1), :], xT[:].rearrange("p g u m -> p g m u"))
            else:
                by_block = grouped[:].rearrange("p g m t -> p (g m t)").bitcast(F32).rearrange(
                    "p (n g m u) -> p n g m u", g=PASSES, m=P, u=2
                )
                copy_out(engine, by_block[:, m], xT[:].rearrange("p g u m -> p g m u"))

        def new_codes():
            codes = work.tile([P, PASSES, SEQ], U32, align_bytes=64)
            planes = work.tile([P, PASSES, SEQ], U8, align_bytes=64)
            return codes, planes

        def quantise(grouped, codes, planes, blocks, m=None):
            flat_in = grouped[:].rearrange("p g m t -> p (g m t)")
            flat_codes = codes[:].rearrange("p g m -> p (g m)")
            flat_planes = planes[:].rearrange("p g m -> p (g m)")
            if blocks == TILES:
                nc.vector.quantize_mx(out=flat_codes.bitcast(FP8X4), scales=flat_planes, in_=flat_in)
            else:
                width = PASSES * P
                nc.vector.quantize_mx(
                    out=flat_codes[:, width * m : width * (m + 1)].bitcast(FP8X4),
                    scales=flat_planes[:, width * m : width * (m + 1)],
                    in_=flat_in[:, PACK * width * m : PACK * width * (m + 1)],
                )

        def new_queries():
            qT = work.tile([P, CHUNKS, SEQ], F32)
            return qT

        def project_chunk(qT, codes, planes, blocks, c):
            acc = psum.tile([P, SEQ], F32, tag="bank")
            flat_codes = codes[:].rearrange("p g m -> p (g m)")
            flat_planes = planes[:].rearrange("p g m -> p (g m)")
            pieces = 1 if blocks == TILES else blocks
            for m in range(pieces):
                for g in range(PASSES):
                    if blocks == TILES:
                        columns = slice(SEQ * g, SEQ * (g + 1))
                        target = acc[:]
                    else:
                        columns = slice(P * (PASSES * m + g), P * (PASSES * m + g + 1))
                        target = acc[:, P * m : P * (m + 1)]
                    nc.tensor.matmul_mx(
                        out=target,
                        lhsT=w_words[:, g, 2 * P * c : 2 * P * (c + 1)].bitcast(FP4X4),
                        lhsT_scale=w_planes[:, g, P * c : P * (c + 1)],
                        rhs=flat_codes[:, columns].bitcast(FP8X4),
                        rhs_scale=flat_planes[:, columns],
                        start=(g == 0),
                        stop=(g == PASSES - 1),
                    )
            nc.scalar.activation(
                out=qT[:, c, 0 : P * blocks],
                in_=acc[:, 0 : P * blocks],
                func=ACT.Identity,
                bias=bias_col[:, c : c + 1],
                scale=-SCORE_SCALE,
            )

        kT_even = keep.tile([P, CHUNKS, PAD + SEQ + PAD], F32)
        kT_odd = keep.tile([P, CHUNKS, PAD + SEQ + PAD], F32)

        def setup_pads():
            for kT in (kT_even, kT_odd):
                nc.gpsimd.memset(kT[:, :, 0:PAD], 0.0)
                nc.gpsimd.memset(kT[:, :, PAD + SEQ : PAD + SEQ + PAD], 0.0)
            short = PAD + P * groups[0][1]
            if short < PAD + SEQ:
                nc.gpsimd.memset(kT_even[:, :, short : short + PAD], 0.0)

        def transpose_keys(kT, first, m, engine="scalar"):
            kT_ps = psum.tile([P, CHUNKS, P], BF16, tag="bank")
            for c in range(CHUNKS):
                nc.tensor.transpose(kT_ps[:, c, :], k_sb[:, first + m - RUN + 1, P * c : P * (c + 1)], ident_bf[:])
            if m < 0:
                copy_out(engine, kT[:, :, PAD - NB : PAD], kT_ps[:, :, P - NB : P])
            else:
                copy_out(engine, kT[:, :, PAD + P * m : PAD + P * (m + 1)], kT_ps[:])

        def band_block(qT, kT, first, m, masked=False):
            block = psum.tile([P, WINDOW], F32, tag="bank")
            first_key = PAD - NB + P * m
            if masked:
                nc.tensor.matmul(out=block[:], lhsT=ident_bf[:], rhs=outside[:], start=True, stop=False)
            for c in range(CHUNKS):
                nc.tensor.matmul(
                    out=block[:],
                    lhsT=qT[:, c, P * m : P * (m + 1)],
                    rhs=kT[:, c, first_key : first_key + WINDOW],
                    start=(c == 0 and not masked),
                    stop=(c == CHUNKS - 1),
                )
            return block

        def band_mask(block, first, m):
            t = first + m
            nc.vector.tensor_mul(
                out=banded[:, t // TILES % 2, t % TILES, :, 0:FOLDS],
                in0=block[:].rearrange("p (a r) -> p r a", r=RESIDUES),
                in1=in_band[:],
            )

        def band_chain(first, blocks, block=None):
            lo = first % TILES
            folded = work.tile([P, TILES, RESIDUES], F32)
            low = work.tile([P, TILES], F32)
            turned = work.tile([P, TILES, REPEATS, RESIDUES], F32)
            total = work.tile([P, TILES], F32)
            share = work.tile([P, TILES, GATHER], F32)
            windows = work.tile([P, TILES, RESIDUES, BAND], F32)
            weights = work.tile([P, TILES, BAND], F32)
            spread = work.tile([P, TILES, GATHER, BAND], F32)
            gathered = work.tile([P, TILES, GATHER, BAND], F32)

            def fold_masked():
                nc.vector.tensor_reduce(out=low[:, 0:1], in_=block[:], axis=AXIS.X, op=ALU.min)
                by_residue = block[:].rearrange("p (a r) -> p r a", r=RESIDUES)
                nc.vector.tensor_reduce(out=folded[:, 0, :], in_=by_residue, axis=AXIS.X, op=ALU.min)

            def fold():
                nc.vector.tensor_reduce(
                    out=folded[:, 0:blocks, :],
                    in_=banded[:, first // TILES % 2, lo : lo + blocks, :, 0 : FOLDS + 1],
                    axis=AXIS.X,
                    op=ALU.add,
                )

            def lowest():
                nc.vector.tensor_reduce(out=low[:, 0:blocks], in_=folded[:, 0:blocks, :], axis=AXIS.X, op=ALU.min)

            def exps():
                for n in range(blocks):
                    nc.scalar.activation(
                        out=turned[:, n, :, :],
                        in_=folded[:, n, :].unsqueeze(1).to_broadcast([P, REPEATS, RESIDUES]),
                        func=ACT.Exp,
                        scale=-1.0,
                        bias=low[:, n : n + 1],
                        accum_out=total[:, n : n + 1],
                    )

            def invert():
                nc.vector.reciprocal(out=total[:, 0:blocks], in_=total[:, 0:blocks])

            def shares():
                nc.vector.tensor_mul(
                    out=share[:, 0:blocks, :],
                    in0=place[:].unsqueeze(1).to_broadcast([P, blocks, GATHER]),
                    in1=total[:, 0:blocks].unsqueeze(2).to_broadcast([P, blocks, GATHER]),
                )

            def turn_back():
                nc.vector.tensor_mul(
                    out=windows[:, 0:blocks],
                    in0=turned[:, 0:blocks]
                    .rearrange("p n a r -> p n (a r)")
                    .rearrange("p n (s c) -> p n s c", c=REPEATS)[:, :, :, 0:BAND],
                    in1=turn[:].unsqueeze(1).unsqueeze(3).to_broadcast([P, blocks, RESIDUES, BAND]),
                )

            def weigh():
                nc.vector.tensor_reduce(
                    out=weights[:, 0:blocks, :],
                    in_=windows[:, 0:blocks].rearrange("p n s j -> p n j s"),
                    axis=AXIS.X,
                    op=ALU.add,
                )

            def spread_out():
                nc.vector.tensor_mul(
                    out=spread[:, 0:blocks],
                    in0=weights[:, 0:blocks, :].unsqueeze(2).to_broadcast([P, blocks, GATHER, BAND]),
                    in1=share[:, 0:blocks, :].unsqueeze(3).to_broadcast([P, blocks, GATHER, BAND]),
                )

            def store():
                gathered_ps = psum.tile([P, TILES, GATHER * BAND], F32, tag="bank")
                nc.tensor.matmul(
                    out=gathered_ps[:, 0:blocks].rearrange("p n c -> p (n c)"),
                    lhsT=pick[:],
                    rhs=spread[:, 0:blocks].rearrange("p n e j -> p (n e j)"),
                    start=True,
                    stop=True,
                )
                rows = P // GATHER
                nc.scalar.copy(
                    out=gathered[0:rows, 0:blocks].rearrange("p n e j -> p (n e j)"),
                    in_=gathered_ps[0:rows, 0:blocks].rearrange("p n c -> p (n c)"),
                )
                store_queue = nc.sync if block is None else nc.scalar
                store_queue.dma_start(
                    out=out_rows[P * first : P * (first + blocks)].rearrange("(n m e) j -> m n (e j)", m=rows, e=GATHER),
                    in_=gathered[0:rows, 0:blocks].rearrange("m n e j -> m n (e j)"),
                )

            if block is not None:
                return [fold_masked, exps, turn_back, invert, shares, weigh, spread_out, store]
            return [fold, lowest, exps, turn_back, invert, shares, weigh, spread_out, store]

        order = sorted(range(RUN), key=lambda i: abs(2 * i - RUN + 1))
        units = [(i, j) for i in order for j in range(BAND)]
        links = []
        run_links = []

        def products(done, count):
            for i, j in units[done : done + count]:
                run_product(i, j)
            if done < len(units) <= done + count:
                run_links.extend(run_chain())
            return done + count

        def share_of(total, parts, index):
            return range(total * index // parts, total * (index + 1) // parts)

        def sort_x(group, m):
            return sort_words(x_sb[:, group[0] + m - RUN, :], "scalar")

        def sort_run(i):
            return sort_words(x_run[:, i, :], "scalar")

        def prepare_x(first, blocks, sorts):
            grouped = new_x()
            codes, planes = new_codes()
            for m in range(blocks):
                transpose_x(grouped, first, blocks, m, "scalar", sorts[m])
                if blocks < TILES:
                    quantise(grouped, codes, planes, blocks, m)
            if blocks == TILES:
                quantise(grouped, codes, planes, blocks)
            return codes, planes

        def project(qT, codes, planes, blocks, chunks=range(CHUNKS)):
            for c in chunks:
                project_chunk(qT, codes, planes, blocks, c)

        def head(i, sort=None):
            run_quantise(i, run_transpose(i, "scalar", sort))

        def project_run(i):
            for h in range(HALVES):
                run_project(i, h)

        filled = []

        def fill(count):
            for i, j in units[len(filled) : len(filled) + count]:
                run_product(i, j)
                filled.append((i, j))

        first, blocks = groups[0]
        with tc.manual_schedule():
            setup_gpsimd()
            setup_pads()
            setup_turn()
            setup_run_mask()
            setup_picks()
            bias_column_scale()
            setup_band()
            head(0)
            head(1)
            for h in range(HALVES):
                bias_row(h)
            bias_column()
            project_run(0)
            sorts = [sort_run(3)]
            head(2)
            head(3, sorts[0])
            sorts = [sort_run(4), sort_run(5)]
            project_run(1)
            project_run(2)
            head(4, sorts[0])
            head(5, sorts[1])
            sorts = [None, sort_x(groups[0], 1)]
            project_run(3)
            codes, planes = prepare_x(first, blocks, sorts)
            second, second_blocks = groups[1]
            project_run(4)
            kT = kT_even
            sorts = [sort_x(groups[1], 0)]
            transpose_keys(kT, first, -1)
            transpose_keys(kT, first, 0)
            sorts.append(sort_x(groups[1], 1))
            project_run(5)
            transpose_keys(kT, first, 1)
            grouped = new_x()
            next_operands = new_codes()
            transpose_x(grouped, second, second_blocks, 0, "scalar", sorts[0])
            transpose_x(grouped, second, second_blocks, 1, "scalar", sorts[1])
            qT = new_queries()
            fill(1)
            project(qT, codes, planes, blocks)
            transpose_x(grouped, second, second_blocks, 2)
            transpose_x(grouped, second, second_blocks, 3)
            fill(4)
            quantise(grouped, *next_operands, second_blocks)

            third, third_blocks = groups[2]
            kT_second = kT_odd
            qT_second = new_queries()
            block = band_block(qT, kT, first, 0)
            transpose_keys(kT_second, second, 0)
            band_mask(block, first, 0)
            fill(2)
            block = band_block(qT, kT, first, 1)
            transpose_keys(kT_second, second, 1)
            transpose_keys(kT_second, second, 2)
            band_mask(block, first, 1)
            chain = band_chain(first, blocks)
            chain[0]()
            fill(1)
            chain[1]()
            project(qT_second, *next_operands, second_blocks, range(0, 4))
            chain[2]()
            project(qT_second, *next_operands, second_blocks, range(4, 8))
            sorts = [sort_x(groups[2], n) for n in range(2)]
            transpose_keys(kT_second, second, 3)
            fill(3)
            chain[3]()
            fill(1)
            chain[4]()
            fill(1)
            chain[5]()

            grouped = new_x()
            codes, planes = new_codes()
            qT_third = new_queries()
            kT_third = kT_even
            block = band_block(qT_second, kT_second, second, 0)
            transpose_x(grouped, third, third_blocks, 0, "scalar", sorts[0])
            transpose_x(grouped, third, third_blocks, 1, "scalar", sorts[1])
            sorts.extend([sort_x(groups[2], n) for n in range(2, 4)])
            chain[6]()
            band_mask(block, second, 0)
            chain[7]()
            block = band_block(qT_second, kT_second, second, 1)
            transpose_x(grouped, third, third_blocks, 2, "scalar", sorts[2])
            transpose_x(grouped, third, third_blocks, 3, "scalar", sorts[3])
            fill(3)
            band_mask(block, second, 1)
            block = band_block(qT_second, kT_second, second, 2)
            chain[8]()
            transpose_keys(kT_third, third, 0)
            transpose_keys(kT_third, third, 1)
            fill(2)
            quantise(grouped, codes, planes, third_blocks)
            band_mask(block, second, 2)
            fill(2)
            block = band_block(qT_second, kT_second, second, 3)
            transpose_keys(kT_third, third, 2)
            band_mask(block, second, 3)
            chain = band_chain(second, second_blocks)
            chain[0]()
            fill(1)
            chain[1]()
            project(qT_third, codes, planes, third_blocks, range(0, 4))
            chain[2]()
            project(qT_third, codes, planes, third_blocks, range(4, 8))
            transpose_keys(kT_third, third, 3)
            fill(3)
            chain[3]()
            fill(1)
            chain[4]()

            block = band_block(qT_third, kT_third, third, 0)
            fill(1)
            chain[5]()
            fill(1)
            chain[6]()
            band_mask(block, third, 0)
            chain[7]()
            block = band_block(qT_third, kT_third, third, 1)
            fill(2)
            band_mask(block, third, 1)
            fill(len(units))
            run_links = run_chain()
            block = band_block(qT_third, kT_third, third, 2)
            band_mask(block, third, 2)
            early = band_chain(third, third_blocks - 1)
            block = band_block(qT_third, kT_third, third, third_blocks - 1, masked=True)
            late = band_chain(third + third_blocks - 1, 1, block)
            run_links[0]()
            early[0]()
            run_links[1]()
            early[1]()
            run_links[2]()
            early[2]()
            run_links[3]()
            late[0]()
            late[1]()
            run_links[4]()
            early[3]()
            run_links[5]()
            early[4]()
            late[2]()
            run_links[6]()
            late[3]()
            early[5]()
            late[5]()
            late[4]()
            early[6]()
            run_links[7]()
            late[6]()
            early[7]()
            chain[8]()
            run_links[8]()
            early[8]()
            late[7]()
